import numpy as np
import ml_dtypes


def mxq(x, axis, fmt="e4m3"):
    dtype, down = {"e4m3": (ml_dtypes.float8_e4m3fn, 7), "e5m2": (ml_dtypes.float8_e5m2, 14)}[fmt]
    v = np.moveaxis(np.asarray(x, np.float32).astype(ml_dtypes.bfloat16).astype(np.float64), axis, -1)
    blocks = v.reshape(v.shape[:-1] + (-1, 32))
    amax = np.abs(blocks).max(-1, keepdims=True)
    byte = np.maximum(np.where(amax > 0, np.frexp(amax)[1] - 1 + 127, 0) - down, 1)
    scale = np.exp2(byte - 127.0)
    codes = (blocks / scale).astype(np.float32).astype(dtype).astype(np.float64)
    return np.moveaxis((codes * scale).reshape(v.shape), -1, axis)


WIDE = False


def mx_kscale(k):
    if not WIDE:
        return np.ones(k)
    levels = np.array([10, -10, 5, -5, 0])
    a = np.random.permutation(np.resize(levels, k // 512 * 4)).reshape(k // 512, 4)
    idx = np.arange(k)
    return np.exp2(a[idx // 512, idx % 128 // 32])


BF16 = ml_dtypes.bfloat16


def bf(x):
    return np.asarray(x, np.float32).astype(BF16)


def f64(x):
    return np.asarray(x).astype(np.float64)


E2M1 = np.array([0.0, 0.5, 1.0, 1.5, 2.0, 3.0, 4.0, 6.0, -0.0, -0.5, -1.0, -1.5, -2.0, -3.0, -4.0, -6.0])


def pack_weight(w, fmt):
    k, n = w.shape
    w = f64(bf(w)).reshape(k // 32, 32, n)
    amax = np.abs(w).max(1)
    if fmt == "e4m3":
        byte = np.frexp(amax)[1] - 1 + 127 - 7
    else:
        mant, ex = np.frexp(amax / 6.0)
        byte = np.where(mant > 0.5, ex, ex - 1) + 127
    byte = np.clip(np.where(amax > 0, byte, 1), 1, 254)
    scaled = (w * np.exp2(127.0 - byte)[:, None, :]).reshape(k, n).astype(np.float32)
    by_word = np.ascontiguousarray(scaled.reshape(k // 512, 128, 4, n).transpose(0, 1, 3, 2))
    if fmt == "e4m3":
        words = by_word.astype(ml_dtypes.float8_e4m3fn).view(np.uint8)
    else:
        c = by_word.astype(ml_dtypes.float4_e2m1fn).view(np.uint8) & 0xF
        words = c[..., 0::2] | (c[..., 1::2] << 4)
    return np.ascontiguousarray(words), np.ascontiguousarray(byte.astype(np.uint8).reshape(k // 512, 16, n))


def unpack_weight(words, scales, fmt):
    g, p, n, _ = words.shape
    if fmt == "e4m3":
        vals = np.ascontiguousarray(words).view(ml_dtypes.float8_e4m3fn).astype(np.float64)
    else:
        nib = np.empty((g, p, n, 4), np.uint8)
        nib[..., 0::2] = words & 0xF
        nib[..., 1::2] = words >> 4
        vals = E2M1[nib]
    vals = vals * np.repeat(np.exp2(scales.astype(np.float64) - 127.0), 8, axis=1)[..., None]
    return vals.transpose(0, 1, 3, 2).reshape(g * 512, n)


B, T, D, H, HKV, HD, R, DFF = 1, 384, 2048, 16, 8, 128, 128, 6144
HALF = HD // 2
EPS = 1e-6
THETA = 1e6
FMT = "e4m3"


def rms_norm(x, w):
    return x / np.sqrt(np.mean(x * x, axis=-1, keepdims=True) + EPS) * w


def rotate_half(x):
    return np.concatenate([-x[..., HALF:], x[..., :HALF]], axis=-1)


def setup_inputs():
    rn = np.random.standard_normal
    s = mx_kscale(D)
    inv_freq = 1.0 / THETA ** (np.arange(HALF) / HALF)
    freqs = np.arange(T)[:, None] * inv_freq[None, :]
    emb = np.concatenate([freqs, freqs], axis=-1)
    hidden_states = bf(rn((B, T, D)) * np.exp(0.5 * rn((B, T, 1))))
    ln1_w = bf((1.0 + 0.1 * rn(D)) * s)
    Wq_words, Wq_scales = pack_weight(rn((D, H * HD)) / np.sqrt(D) / s[:, None], FMT)
    Wk_words, Wk_scales = pack_weight(rn((D, HKV * HD)) / np.sqrt(D) / s[:, None], FMT)
    Wv_words, Wv_scales = pack_weight(rn((D, HKV * HD)) / np.sqrt(D) / s[:, None], FMT)
    q_norm_w = bf(1.0 + 0.1 * rn(HD))
    k_norm_w = bf(1.0 + 0.1 * rn(HD))
    return {
        "hidden_states": hidden_states,
        "ln1_w": ln1_w,
        "Wq_words": Wq_words,
        "Wq_scales": Wq_scales,
        "Wk_words": Wk_words,
        "Wk_scales": Wk_scales,
        "Wv_words": Wv_words,
        "Wv_scales": Wv_scales,
        "q_norm_w": q_norm_w,
        "k_norm_w": k_norm_w,
        "cos": bf(np.cos(emb)),
        "sin": bf(np.sin(emb)),
    }


def reference(hidden_states, ln1_w, Wq_words, Wq_scales, Wk_words, Wk_scales, Wv_words, Wv_scales, q_norm_w, k_norm_w, cos, sin):
    h = rms_norm(f64(hidden_states), f64(ln1_w))
    hq = mxq(h, 2, "e4m3")
    q = rms_norm((hq @ unpack_weight(Wq_words, Wq_scales, FMT)).reshape(B, T, H, HD), f64(q_norm_w)).transpose(0, 2, 1, 3)
    k = rms_norm((hq @ unpack_weight(Wk_words, Wk_scales, FMT)).reshape(B, T, HKV, HD), f64(k_norm_w)).transpose(0, 2, 1, 3)
    v = (hq @ unpack_weight(Wv_words, Wv_scales, FMT)).reshape(B, T, HKV, HD).transpose(0, 2, 1, 3)
    c, s_ = f64(cos)[None, None], f64(sin)[None, None]
    q = q * c + rotate_half(q) * s_
    k = k * c + rotate_half(k) * s_
    return q, k, v

@@ -1,0 +1,246 @@
+from contextlib import ExitStack
+
+import concourse.mybir as mybir
+from concourse.masks import make_identity
+
+F32 = mybir.dt.float32
+BF16 = mybir.dt.bfloat16
+I32 = mybir.dt.int32
+U32 = mybir.dt.uint32
+U8 = mybir.dt.uint8
+FP8X4 = mybir.dt.float8_e4m3fn_x4
+ALU = mybir.AluOpType
+ACT = mybir.ActivationFunctionType
+
+P = 128
+PACK = 4
+K_PASS = P * PACK
+TOKENS = 384
+D_MODEL = 2048
+HEAD = 128
+HALF = HEAD // 2
+EPS = 1e-6
+TILES = TOKENS // P
+PASSES = D_MODEL // K_PASS
+N_BLOCK = 512
+HEADS = N_BLOCK // HEAD
+N_ALL = 4096
+QUADRANT = 32
+LIVE = PASSES * 4
+ROUND = 2
+
+FLOPS = 2 * TOKENS * D_MODEL * N_ALL
+
+
+def tile_rawkvinjector_pa_kernel(
+    tc,
+    hidden_states,
+    ln1_w,
+    Wq_words,
+    Wq_scales,
+    Wk_words,
+    Wk_scales,
+    Wv_words,
+    Wv_scales,
+    q_norm_w,
+    k_norm_w,
+    cos,
+    sin,
+    out_0,
+    out_1,
+    out_2,
+):
+    nc = tc.nc
+    projections = (
+        (Wq_words, Wq_scales, out_0, 0),
+        (Wk_words, Wk_scales, out_1, 1),
+        (Wv_words, Wv_scales, out_2, None),
+    )
+
+    with ExitStack() as ctx:
+        keep = ctx.enter_context(tc.tile_pool(name="keep", bufs=1))
+        stage = ctx.enter_context(tc.tile_pool(name="stage", bufs=2))
+        small = ctx.enter_context(tc.tile_pool(name="small", bufs=4))
+        results = ctx.enter_context(tc.tile_pool(name="results", bufs=2 * ROUND))
+        turned = ctx.enter_context(tc.psum_pool(name="turned", bufs=2))
+        sums = ctx.enter_context(tc.psum_pool(name="sums", bufs=6))
+
+        eps = keep.tile([P, 1], F32)
+        nc.vector.memset(eps[:], EPS)
+        table_warm = keep.tile([P, 1], F32)
+        nc.scalar.activation(out=table_warm[:], in_=eps[:], func=ACT.Sqrt)
+        identity = keep.tile([P, P], F32)
+        make_identity(nc, identity[:])
+
+        x_all = keep.tile([P, TILES, D_MODEL], BF16)
+        x_rows = hidden_states.rearrange("b (p m) k -> p (b m) k", m=TILES)
+        for m in range(TILES):
+            nc.sync.dma_start(out=x_all[:, m, :], in_=x_rows[:, m, :])
+
+        w_planes = keep.tile([P, N_ALL], U8, align_bytes=64)
+        nc.vector.memset(w_planes[:].bitcast(I32), 0)
+        first_col = 0
+        for words, scales, out, norm in projections:
+            n_cols = scales.shape[2]
+            for quad in range(P // QUADRANT):
+                nc.sync.dma_start(
+                    out=w_planes[
+                        quad * QUADRANT : quad * QUADRANT + LIVE, first_col : first_col + n_cols
+                    ].bitcast(I32),
+                    in_=scales[:, 4 * quad : 4 * quad + 4, :].bitcast(I32),
+                )
+            first_col += n_cols
+
+        ln_w = keep.tile([P, PASSES, PACK], BF16)
+        nc.scalar.dma_start(out=ln_w[:], in_=ln1_w.rearrange("(g p t) -> p g t", p=P, t=PACK))
+        cos_rows = keep.tile([P, TILES, HEAD], BF16)
+        nc.scalar.dma_start(out=cos_rows[:], in_=cos.rearrange("(p m) d -> p m d", m=TILES))
+        sin_rows = keep.tile([P, TILES, HEAD], BF16)
+        nc.scalar.dma_start(out=sin_rows[:], in_=sin.rearrange("(p m) d -> p m d", m=TILES))
+        norm_w = keep.tile([P, 2, HEAD], BF16)
+        nc.gpsimd.dma_start(out=norm_w[:, 0, :], in_=q_norm_w.partition_broadcast(P))
+        nc.gpsimd.dma_start(out=norm_w[:, 1, :], in_=k_norm_w.partition_broadcast(P))
+
+        blocks = []
+        first_col = 0
+        for words, scales, out, norm in projections:
+            bytes_by_pass = words.rearrange("g p n t -> p g (n t)")
+            for n0 in range(0, words.shape[2], N_BLOCK):
+                w_words = keep.tile([P, PASSES, N_BLOCK], U32, name="w_words%d" % first_col, align_bytes=64)
+                nc.sync.dma_start(
+                    out=w_words[:].bitcast(I32),
+                    in_=bytes_by_pass[:, :, PACK * n0 : PACK * (n0 + N_BLOCK)].bitcast(I32),
+                )
+                blocks.append((w_words, first_col, out, n0 // HEAD, norm))
+                first_col += N_BLOCK
+
+        rope = []
+        for norm in range(2):
+            table = keep.tile([P, TILES, 2, HEAD], F32, name="rope%d" % norm)
+            w_all = norm_w[:, norm, :].unsqueeze(1)
+            nc.vector.tensor_tensor(
+                out=table[:, :, 0, :], in0=cos_rows[:], in1=w_all.to_broadcast([P, TILES, HEAD]), op=ALU.mult
+            )
+            nc.vector.tensor_tensor(
+                out=table[:, :, 1, :HALF],
+                in0=sin_rows[:, :, HALF:],
+                in1=w_all[:, :, :HALF].to_broadcast([P, TILES, HALF]),
+                op=ALU.mult,
+            )
+            nc.vector.tensor_tensor(
+                out=table[:, :, 1, HALF:],
+                in0=sin_rows[:, :, :HALF],
+                in1=w_all[:, :, HALF:].to_broadcast([P, TILES, HALF]),
+                op=ALU.mult,
+            )
+            rope.append(table)
+
+        h_words = keep.tile([P, TILES, PASSES * P], U32, align_bytes=64)
+        h_planes = keep.tile([P, TILES, PASSES * P], U8, align_bytes=64)
+        x_sumsq = keep.tile([P, TILES], F32)
+        x_rms = keep.tile([P, TILES], F32)
+        x_rinv = keep.tile([P, TILES], F32)
+        for m in range(TILES):
+            squares = stage.tile([P, D_MODEL], BF16)
+            nc.scalar.activation(
+                out=squares[:], in_=x_all[:, m, :], func=ACT.Square, accum_out=x_sumsq[:, m : m + 1]
+            )
+            nc.scalar.activation(
+                out=x_rms[:, m : m + 1],
+                in_=x_sumsq[:, m : m + 1],
+                func=ACT.Sqrt,
+                scale=1.0 / D_MODEL,
+                bias=eps[:],
+            )
+            nc.vector.reciprocal(out=x_rinv[:, m : m + 1], in_=x_rms[:, m : m + 1])
+
+            grouped = stage.tile([P, PASSES, P, PACK], BF16, align_bytes=64)
+            for g in range(PASSES):
+                scaled = stage.tile([P, PACK, P], F32, bufs=4)
+                nc.gpsimd.tensor_scalar(
+                    out=scaled[:],
+                    in0=x_all[:, m, g * K_PASS : (g + 1) * K_PASS].rearrange("r (p t) -> r t p", t=PACK),
+                    scalar1=x_rinv[:, m : m + 1],
+                    scalar2=0.0,
+                    op0=ALU.mult,
+                    op1=ALU.add,
+                )
+                flipped = turned.tile([P, PACK, P], F32)
+                for t in range(PACK):
+                    nc.tensor.transpose(flipped[:, t, :], scaled[:, t, :], identity[:])
+                nc.vector.tensor_tensor(
+                    out=grouped[:, g],
+                    in0=flipped[:].rearrange("p t r -> p r t"),
+                    in1=ln_w[:, g, :].unsqueeze(1).to_broadcast([P, P, PACK]),
+                    op=ALU.mult,
+                )
+            nc.vector.quantize_mx(
+                out=h_words[:, m, :].bitcast(FP8X4),
+                scales=h_planes[:, m, :],
+                in_=grouped[:].rearrange("p g r t -> p (g r t)"),
+            )
+
+        for first_block in range(0, len(blocks), ROUND):
+            round_blocks = blocks[first_block : first_block + ROUND]
+            round_results = []
+            for i in range(ROUND):
+                finished = results.tile([P, HEADS, TILES, HEAD], F32)
+                round_results.append(finished)
+            for m in range(TILES):
+                for (w_words, first_col, out, first_head, norm), finished in zip(round_blocks, round_results):
+                    product = sums.tile([P, HEADS, HEAD], F32)
+                    for g in range(PASSES):
+                        nc.tensor.matmul_mx(
+                            out=product[:].rearrange("p h d -> p (h d)"),
+                            lhsT=h_words[:, m, g * P : (g + 1) * P].bitcast(FP8X4),
+                            lhsT_scale=h_planes[:, m, g * P : (g + 1) * P],
+                            rhs=w_words[:, g, :].bitcast(FP8X4),
+                            rhs_scale=w_planes[4 * g : P, first_col : first_col + N_BLOCK],
+                            start=(g == 0),
+                            stop=(g == PASSES - 1),
+                        )
+                    if norm is None:
+                        nc.scalar.copy(out=finished[:, :, m, :], in_=product[:])
+                    else:
+                        head_sumsq = small.tile([P, HEADS], F32)
+                        head_squares = stage.tile([P, HEADS, HEAD], BF16)
+                        for h in range(HEADS):
+                            nc.scalar.activation(
+                                out=head_squares[:, h, :],
+                                in_=product[:, h, :],
+                                func=ACT.Square,
+                                accum_out=head_sumsq[:, h : h + 1],
+                            )
+                        head_rms = small.tile([P, HEADS], F32)
+                        nc.scalar.activation(
+                            out=head_rms[:], in_=head_sumsq[:], func=ACT.Sqrt, scale=1.0 / HEAD, bias=eps[:]
+                        )
+                        head_rinv = small.tile([P, HEADS], F32)
+                        nc.vector.reciprocal(out=head_rinv[:], in_=head_rms[:])
+                        terms = stage.tile([P, HEADS, 2, HEAD], F32, bufs=6)
+                        for h in range(HEADS):
+                            nc.vector.scalar_tensor_tensor(
+                                out=terms[:, h],
+                                in0=product[:, h, :].unsqueeze(1).to_broadcast([P, 2, HEAD]),
+                                scalar=head_rinv[:, h : h + 1],
+                                in1=rope[norm][:, m],
+                                op0=ALU.mult,
+                                op1=ALU.mult,
+                            )
+                        nc.gpsimd.tensor_tensor(
+                            out=finished[:, :, m, :HALF],
+                            in0=terms[:, :, 0, :HALF],
+                            in1=terms[:, :, 1, HALF:],
+                            op=ALU.subtract,
+                        )
+                        nc.gpsimd.tensor_tensor(
+                            out=finished[:, :, m, HALF:],
+                            in0=terms[:, :, 0, HALF:],
+                            in1=terms[:, :, 1, :HALF],
+                            op=ALU.add,
+                        )
+            for (w_words, first_col, out, first_head, norm), finished in zip(round_blocks, round_results):
+                nc.sync.dma_start(
+                    out=out.rearrange("b h (p m) d -> p (b h) (m d)", m=TILES)[:, first_head : first_head + HEADS, :],
+                    in_=finished[:].rearrange("p h m d -> p h (m d)"),
+                )

@@ -27,7 +27,7 @@ HEADS = N_BLOCK // HEAD
 N_ALL = 4096
 QUADRANT = 32
 LIVE = PASSES * 4
-ROUND = 2
+HALF_PASSES = PASSES // 2
 
 FLOPS = 2 * TOKENS * D_MODEL * N_ALL
 
@@ -61,7 +61,7 @@ def tile_rawkvinjector_pa_kernel(
         keep = ctx.enter_context(tc.tile_pool(name="keep", bufs=1))
         stage = ctx.enter_context(tc.tile_pool(name="stage", bufs=2))
         small = ctx.enter_context(tc.tile_pool(name="small", bufs=4))
-        results = ctx.enter_context(tc.tile_pool(name="results", bufs=2 * ROUND))
+        results = ctx.enter_context(tc.tile_pool(name="results", bufs=N_ALL // N_BLOCK))
         turned = ctx.enter_context(tc.psum_pool(name="turned", bufs=2))
         sums = ctx.enter_context(tc.psum_pool(name="sums", bufs=6))
 
@@ -127,11 +127,13 @@ def tile_rawkvinjector_pa_kernel(
                 in1=w_all[:, :, :HALF].to_broadcast([P, TILES, HALF]),
                 op=ALU.mult,
             )
-            nc.vector.tensor_tensor(
+            nc.vector.scalar_tensor_tensor(
                 out=table[:, :, 1, HALF:],
                 in0=sin_rows[:, :, :HALF],
+                scalar=-1.0,
                 in1=w_all[:, :, HALF:].to_broadcast([P, TILES, HALF]),
-                op=ALU.mult,
+                op0=ALU.mult,
+                op1=ALU.mult,
             )
             rope.append(table)
 
@@ -155,92 +157,84 @@ def tile_rawkvinjector_pa_kernel(
             nc.vector.reciprocal(out=x_rinv[:, m : m + 1], in_=x_rms[:, m : m + 1])
 
             grouped = stage.tile([P, PASSES, P, PACK], BF16, align_bytes=64)
-            for g in range(PASSES):
-                scaled = stage.tile([P, PACK, P], F32, bufs=4)
+            for first_pass in range(0, PASSES, HALF_PASSES):
+                scaled = stage.tile([P, HALF_PASSES, PACK, P], F32, bufs=3)
                 nc.gpsimd.tensor_scalar(
                     out=scaled[:],
-                    in0=x_all[:, m, g * K_PASS : (g + 1) * K_PASS].rearrange("r (p t) -> r t p", t=PACK),
+                    in0=x_all[:, m, first_pass * K_PASS : (first_pass + HALF_PASSES) * K_PASS].rearrange(
+                        "r (g p t) -> r g t p", p=P, t=PACK
+                    ),
                     scalar1=x_rinv[:, m : m + 1],
                     scalar2=0.0,
                     op0=ALU.mult,
                     op1=ALU.add,
                 )
-                flipped = turned.tile([P, PACK, P], F32)
-                for t in range(PACK):
-                    nc.tensor.transpose(flipped[:, t, :], scaled[:, t, :], identity[:])
-                nc.vector.tensor_tensor(
-                    out=grouped[:, g],
-                    in0=flipped[:].rearrange("p t r -> p r t"),
-                    in1=ln_w[:, g, :].unsqueeze(1).to_broadcast([P, P, PACK]),
-                    op=ALU.mult,
-                )
+                for i in range(HALF_PASSES):
+                    g = first_pass + i
+                    flipped = turned.tile([P, PACK, P], F32)
+                    for t in range(PACK):
+                        nc.tensor.transpose(flipped[:, t, :], scaled[:, i, t, :], identity[:])
+                    nc.vector.tensor_tensor(
+                        out=grouped[:, g],
+                        in0=flipped[:].rearrange("p t r -> p r t"),
+                        in1=ln_w[:, g, :].unsqueeze(1).to_broadcast([P, P, PACK]),
+                        op=ALU.mult,
+                    )
             nc.vector.quantize_mx(
                 out=h_words[:, m, :].bitcast(FP8X4),
                 scales=h_planes[:, m, :],
                 in_=grouped[:].rearrange("p g r t -> p (g r t)"),
             )
 
-        for first_block in range(0, len(blocks), ROUND):
-            round_blocks = blocks[first_block : first_block + ROUND]
-            round_results = []
-            for i in range(ROUND):
-                finished = results.tile([P, HEADS, TILES, HEAD], F32)
-                round_results.append(finished)
+        for w_words, first_col, out, first_head, norm in blocks:
+            finished = results.tile([P, HEADS, TILES, HEAD], F32)
             for m in range(TILES):
-                for (w_words, first_col, out, first_head, norm), finished in zip(round_blocks, round_results):
-                    product = sums.tile([P, HEADS, HEAD], F32)
-                    for g in range(PASSES):
-                        nc.tensor.matmul_mx(
-                            out=product[:].rearrange("p h d -> p (h d)"),
-                            lhsT=h_words[:, m, g * P : (g + 1) * P].bitcast(FP8X4),
-                            lhsT_scale=h_planes[:, m, g * P : (g + 1) * P],
-                            rhs=w_words[:, g, :].bitcast(FP8X4),
-                            rhs_scale=w_planes[4 * g : P, first_col : first_col + N_BLOCK],
-                            start=(g == 0),
-                            stop=(g == PASSES - 1),
-                        )
-                    if norm is None:
-                        nc.scalar.copy(out=finished[:, :, m, :], in_=product[:])
-                    else:
-                        head_sumsq = small.tile([P, HEADS], F32)
-                        head_squares = stage.tile([P, HEADS, HEAD], BF16)
-                        for h in range(HEADS):
-                            nc.scalar.activation(
-                                out=head_squares[:, h, :],
-                                in_=product[:, h, :],
-                                func=ACT.Square,
-                                accum_out=head_sumsq[:, h : h + 1],
-                            )
-                        head_rms = small.tile([P, HEADS], F32)
+                product = sums.tile([P, HEADS, HEAD], F32)
+                for g in range(PASSES):
+                    nc.tensor.matmul_mx(
+                        out=product[:].rearrange("p h d -> p (h d)"),
+                        lhsT=h_words[:, m, g * P : (g + 1) * P].bitcast(FP8X4),
+                        lhsT_scale=h_planes[:, m, g * P : (g + 1) * P],
+                        rhs=w_words[:, g, :].bitcast(FP8X4),
+                        rhs_scale=w_planes[4 * g : P, first_col : first_col + N_BLOCK],
+                        start=(g == 0),
+                        stop=(g == PASSES - 1),
+                    )
+                if norm is None:
+                    nc.scalar.copy(out=finished[:, :, m, :], in_=product[:])
+                else:
+                    head_sumsq = small.tile([P, HEADS], F32)
+                    head_squares = stage.tile([P, HEADS, HEAD], BF16)
+                    for h in range(HEADS):
                         nc.scalar.activation(
-                            out=head_rms[:], in_=head_sumsq[:], func=ACT.Sqrt, scale=1.0 / HEAD, bias=eps[:]
+                            out=head_squares[:, h, :],
+                            in_=product[:, h, :],
+                            func=ACT.Square,
+                            accum_out=head_sumsq[:, h : h + 1],
                         )
-                        head_rinv = small.tile([P, HEADS], F32)
-                        nc.vector.reciprocal(out=head_rinv[:], in_=head_rms[:])
-                        terms = stage.tile([P, HEADS, 2, HEAD], F32, bufs=6)
-                        for h in range(HEADS):
-                            nc.vector.scalar_tensor_tensor(
-                                out=terms[:, h],
-                                in0=product[:, h, :].unsqueeze(1).to_broadcast([P, 2, HEAD]),
-                                scalar=head_rinv[:, h : h + 1],
-                                in1=rope[norm][:, m],
-                                op0=ALU.mult,
-                                op1=ALU.mult,
-                            )
-                        nc.gpsimd.tensor_tensor(
-                            out=finished[:, :, m, :HALF],
-                            in0=terms[:, :, 0, :HALF],
-                            in1=terms[:, :, 1, HALF:],
-                            op=ALU.subtract,
+                    head_rms = small.tile([P, HEADS], F32)
+                    nc.scalar.activation(
+                        out=head_rms[:], in_=head_sumsq[:], func=ACT.Sqrt, scale=1.0 / HEAD, bias=eps[:]
+                    )
+                    head_rinv = small.tile([P, HEADS], F32)
+                    nc.vector.reciprocal(out=head_rinv[:], in_=head_rms[:])
+                    terms = stage.tile([P, HEADS, 2, HEAD], F32, bufs=6)
+                    for h in range(HEADS):
+                        nc.vector.scalar_tensor_tensor(
+                            out=terms[:, h],
+                            in0=product[:, h, :].unsqueeze(1).to_broadcast([P, 2, HEAD]),
+                            scalar=head_rinv[:, h : h + 1],
+                            in1=rope[norm][:, m],
+                            op0=ALU.mult,
+                            op1=ALU.mult,
                         )
-                        nc.gpsimd.tensor_tensor(
-                            out=finished[:, :, m, HALF:],
-                            in0=terms[:, :, 0, HALF:],
-                            in1=terms[:, :, 1, :HALF],
-                            op=ALU.add,
-                        )
-            for (w_words, first_col, out, first_head, norm), finished in zip(round_blocks, round_results):
-                nc.sync.dma_start(
-                    out=out.rearrange("b h (p m) d -> p (b h) (m d)", m=TILES)[:, first_head : first_head + HEADS, :],
-                    in_=finished[:].rearrange("p h m d -> p h (m d)"),
-                )
+                    nc.gpsimd.tensor_tensor(
+                        out=finished[:, :, m, :].rearrange("p h (s j) -> p h s j", s=2),
+                        in0=terms[:, :, 0, :].rearrange("p h (s j) -> p h s j", s=2),
+                        in1=terms[:, :, 1, :].rearrange("p h (s j) -> p h s j", s=2)[:, :, ::-1, :],
+                        op=ALU.add,
+                    )
+            nc.sync.dma_start(
+                out=out.rearrange("b h (p m) d -> p (b h) (m d)", m=TILES)[:, first_head : first_head + HEADS, :],
+                in_=finished[:].rearrange("p h m d -> p h (m d)"),
+            )

@@ -228,7 +228,7 @@ def tile_rawkvinjector_pa_kernel(
                             op0=ALU.mult,
                             op1=ALU.mult,
                         )
-                    nc.gpsimd.tensor_tensor(
+                    nc.vector.tensor_tensor(
                         out=finished[:, :, m, :].rearrange("p h (s j) -> p h s j", s=2),
                         in0=terms[:, :, 0, :].rearrange("p h (s j) -> p h s j", s=2),
                         in1=terms[:, :, 1, :].rearrange("p h (s j) -> p h s j", s=2)[:, :, ::-1, :],

@@ -27,7 +27,7 @@ HEADS = N_BLOCK // HEAD
 N_ALL = 4096
 QUADRANT = 32
 LIVE = PASSES * 4
-HALF_PASSES = PASSES // 2
+PAIR = 2
 
 FLOPS = 2 * TOKENS * D_MODEL * N_ALL
 
@@ -65,13 +65,6 @@ def tile_rawkvinjector_pa_kernel(
         turned = ctx.enter_context(tc.psum_pool(name="turned", bufs=2))
         sums = ctx.enter_context(tc.psum_pool(name="sums", bufs=6))
 
-        eps = keep.tile([P, 1], F32)
-        nc.vector.memset(eps[:], EPS)
-        table_warm = keep.tile([P, 1], F32)
-        nc.scalar.activation(out=table_warm[:], in_=eps[:], func=ACT.Sqrt)
-        identity = keep.tile([P, P], F32)
-        make_identity(nc, identity[:])
-
         x_all = keep.tile([P, TILES, D_MODEL], BF16)
         x_rows = hidden_states.rearrange("b (p m) k -> p (b m) k", m=TILES)
         for m in range(TILES):
@@ -79,17 +72,17 @@ def tile_rawkvinjector_pa_kernel(
 
         w_planes = keep.tile([P, N_ALL], U8, align_bytes=64)
         nc.vector.memset(w_planes[:].bitcast(I32), 0)
-        first_col = 0
+        plane_col = 0
         for words, scales, out, norm in projections:
             n_cols = scales.shape[2]
             for quad in range(P // QUADRANT):
                 nc.sync.dma_start(
                     out=w_planes[
-                        quad * QUADRANT : quad * QUADRANT + LIVE, first_col : first_col + n_cols
+                        quad * QUADRANT : quad * QUADRANT + LIVE, plane_col : plane_col + n_cols
                     ].bitcast(I32),
                     in_=scales[:, 4 * quad : 4 * quad + 4, :].bitcast(I32),
                 )
-            first_col += n_cols
+            plane_col += n_cols
 
         ln_w = keep.tile([P, PASSES, PACK], BF16)
         nc.scalar.dma_start(out=ln_w[:], in_=ln1_w.rearrange("(g p t) -> p g t", p=P, t=PACK))
@@ -97,23 +90,40 @@ def tile_rawkvinjector_pa_kernel(
         nc.scalar.dma_start(out=cos_rows[:], in_=cos.rearrange("(p m) d -> p m d", m=TILES))
         sin_rows = keep.tile([P, TILES, HEAD], BF16)
         nc.scalar.dma_start(out=sin_rows[:], in_=sin.rearrange("(p m) d -> p m d", m=TILES))
-        norm_w = keep.tile([P, 2, HEAD], BF16)
-        nc.gpsimd.dma_start(out=norm_w[:, 0, :], in_=q_norm_w.partition_broadcast(P))
-        nc.gpsimd.dma_start(out=norm_w[:, 1, :], in_=k_norm_w.partition_broadcast(P))
+        norm_rows = keep.tile([P, 2 * HEAD], BF16)
+        nc.vector.memset(norm_rows[:].bitcast(I32), 0)
+        nc.scalar.dma_start(out=norm_rows[0:1, :HEAD], in_=q_norm_w.unsqueeze(0))
+        nc.scalar.dma_start(out=norm_rows[0:1, HEAD:], in_=k_norm_w.unsqueeze(0))
 
         blocks = []
-        first_col = 0
+        plane_col = 0
         for words, scales, out, norm in projections:
-            bytes_by_pass = words.rearrange("g p n t -> p g (n t)")
-            for n0 in range(0, words.shape[2], N_BLOCK):
-                w_words = keep.tile([P, PASSES, N_BLOCK], U32, name="w_words%d" % first_col, align_bytes=64)
-                nc.sync.dma_start(
-                    out=w_words[:].bitcast(I32),
-                    in_=bytes_by_pass[:, :, PACK * n0 : PACK * (n0 + N_BLOCK)].bitcast(I32),
-                )
-                blocks.append((w_words, first_col, out, n0 // HEAD, norm))
-                first_col += N_BLOCK
+            for n0 in range(0, words.shape[2], PAIR * N_BLOCK):
+                w_words = keep.tile([P, PASSES, PAIR * N_BLOCK], U32, name="w_words%d" % plane_col, align_bytes=64)
+                for g in range(PASSES):
+                    nc.sync.dma_start(
+                        out=w_words[:, g, :].bitcast(I32),
+                        in_=words[g]
+                        .rearrange("p n t -> p (n t)")[:, PACK * n0 : PACK * (n0 + PAIR * N_BLOCK)]
+                        .bitcast(I32),
+                    )
+                for i in range(PAIR):
+                    blocks.append((w_words, i * N_BLOCK, plane_col, out, (n0 + i * N_BLOCK) // HEAD, norm))
+                    plane_col += N_BLOCK
 
+        eps = keep.tile([P, 1], F32)
+        nc.vector.memset(eps[:], EPS)
+        table_warm = keep.tile([P, 1], F32)
+        nc.scalar.activation(out=table_warm[:], in_=eps[:], func=ACT.Sqrt)
+        identity = keep.tile([P, P], F32)
+        make_identity(nc, identity[:])
+        ones = keep.tile([P, P], BF16)
+        nc.vector.memset(ones[:], 1.0)
+
+        norm_w = turned.tile([P, 2, HEAD], F32, tag="flipped")
+        nc.tensor.matmul(
+            out=norm_w[:].rearrange("p n d -> p (n d)"), lhsT=ones[:], rhs=norm_rows[:], start=True, stop=True
+        )
         rope = []
         for norm in range(2):
             table = keep.tile([P, TILES, 2, HEAD], F32, name="rope%d" % norm)
@@ -137,11 +147,20 @@ def tile_rawkvinjector_pa_kernel(
             )
             rope.append(table)
 
-        h_words = keep.tile([P, TILES, PASSES * P], U32, align_bytes=64)
-        h_planes = keep.tile([P, TILES, PASSES * P], U8, align_bytes=64)
+        h_words = keep.tile([P, TILES, PASSES, P], U32, align_bytes=64)
+        h_planes = keep.tile([P, TILES, PASSES, P], U8, align_bytes=64)
         x_sumsq = keep.tile([P, TILES], F32)
         x_rms = keep.tile([P, TILES], F32)
         x_rinv = keep.tile([P, TILES], F32)
+        def quantise(chunk):
+            m, g, grouped = chunk
+            nc.vector.quantize_mx(
+                out=h_words[:, m, g, :].bitcast(FP8X4),
+                scales=h_planes[:, m, g, :],
+                in_=grouped[:].rearrange("p r t -> p (r t)"),
+            )
+
+        copied = None
         for m in range(TILES):
             squares = stage.tile([P, D_MODEL], BF16)
             nc.scalar.activation(
@@ -155,86 +174,121 @@ def tile_rawkvinjector_pa_kernel(
                 bias=eps[:],
             )
             nc.vector.reciprocal(out=x_rinv[:, m : m + 1], in_=x_rms[:, m : m + 1])
-
-            grouped = stage.tile([P, PASSES, P, PACK], BF16, align_bytes=64)
-            for first_pass in range(0, PASSES, HALF_PASSES):
-                scaled = stage.tile([P, HALF_PASSES, PACK, P], F32, bufs=3)
-                nc.gpsimd.tensor_scalar(
-                    out=scaled[:],
-                    in0=x_all[:, m, first_pass * K_PASS : (first_pass + HALF_PASSES) * K_PASS].rearrange(
-                        "r (g p t) -> r g t p", p=P, t=PACK
-                    ),
-                    scalar1=x_rinv[:, m : m + 1],
-                    scalar2=0.0,
-                    op0=ALU.mult,
-                    op1=ALU.add,
-                )
-                for i in range(HALF_PASSES):
-                    g = first_pass + i
-                    flipped = turned.tile([P, PACK, P], F32)
-                    for t in range(PACK):
-                        nc.tensor.transpose(flipped[:, t, :], scaled[:, i, t, :], identity[:])
-                    nc.vector.tensor_tensor(
-                        out=grouped[:, g],
-                        in0=flipped[:].rearrange("p t r -> p r t"),
-                        in1=ln_w[:, g, :].unsqueeze(1).to_broadcast([P, P, PACK]),
-                        op=ALU.mult,
+            for g in range(PASSES):
+                scaled = stage.tile([P, PACK, P], F32, bufs=4)
+                sorted_x = x_all[:, m, g * K_PASS : (g + 1) * K_PASS].rearrange("r (p t) -> r t p", t=PACK)
+                if g < PASSES - 1:
+                    nc.gpsimd.tensor_scalar(
+                        out=scaled[:],
+                        in0=sorted_x,
+                        scalar1=x_rinv[:, m : m + 1],
+                        scalar2=0.0,
+                        op0=ALU.mult,
+                        op1=ALU.add,
                     )
-            nc.vector.quantize_mx(
-                out=h_words[:, m, :].bitcast(FP8X4),
-                scales=h_planes[:, m, :],
-                in_=grouped[:].rearrange("p g r t -> p (g r t)"),
-            )
+                else:
+                    nc.scalar.activation(out=scaled[:], in_=sorted_x, func=ACT.Copy, scale=x_rinv[:, m : m + 1])
+                flipped = turned.tile([P, PACK, P], F32)
+                for t in range(PACK):
+                    nc.tensor.transpose(flipped[:, t, :], scaled[:, t, :], identity[:])
+                grouped = stage.tile([P, P, PACK], BF16, bufs=4, align_bytes=64)
+                nc.vector.tensor_tensor(
+                    out=grouped[:],
+                    in0=flipped[:].rearrange("p t r -> p r t"),
+                    in1=ln_w[:, g, :].unsqueeze(1).to_broadcast([P, P, PACK]),
+                    op=ALU.mult,
+                )
+                if copied is not None:
+                    quantise(copied)
+                copied = (m, g, grouped)
+        quantise(copied)
 
-        for w_words, first_col, out, first_head, norm in blocks:
-            finished = results.tile([P, HEADS, TILES, HEAD], F32)
-            for m in range(TILES):
+        finished = {}
+        last_rope_col = max(block[2] for block in blocks if block[5] is not None)
+
+        def products_and_norms(group, m):
+            norm = group[0][5]
+            products = []
+            for block in group:
                 product = sums.tile([P, HEADS, HEAD], F32)
-                for g in range(PASSES):
+                products.append(product)
+                if m == 0:
+                    result = results.tile([P, HEADS, TILES, HEAD], F32)
+                    finished[block[2]] = result
+            for g in range(PASSES):
+                for block, product in zip(group, products):
+                    w_words, words_col, plane_col = block[0], block[1], block[2]
                     nc.tensor.matmul_mx(
                         out=product[:].rearrange("p h d -> p (h d)"),
-                        lhsT=h_words[:, m, g * P : (g + 1) * P].bitcast(FP8X4),
-                        lhsT_scale=h_planes[:, m, g * P : (g + 1) * P],
-                        rhs=w_words[:, g, :].bitcast(FP8X4),
-                        rhs_scale=w_planes[4 * g : P, first_col : first_col + N_BLOCK],
+                        lhsT=h_words[:, m, g, :].bitcast(FP8X4),
+                        lhsT_scale=h_planes[:, m, g, :],
+                        rhs=w_words[:, g, words_col : words_col + N_BLOCK].bitcast(FP8X4),
+                        rhs_scale=w_planes[4 * g : P, plane_col : plane_col + N_BLOCK],
                         start=(g == 0),
                         stop=(g == PASSES - 1),
                     )
-                if norm is None:
-                    nc.scalar.copy(out=finished[:, :, m, :], in_=product[:])
-                else:
-                    head_sumsq = small.tile([P, HEADS], F32)
-                    head_squares = stage.tile([P, HEADS, HEAD], BF16)
-                    for h in range(HEADS):
-                        nc.scalar.activation(
-                            out=head_squares[:, h, :],
-                            in_=product[:, h, :],
-                            func=ACT.Square,
-                            accum_out=head_sumsq[:, h : h + 1],
-                        )
-                    head_rms = small.tile([P, HEADS], F32)
+            if norm is None:
+                for block, product in zip(group, products):
+                    nc.scalar.copy(out=finished[block[2]][:, :, m, :], in_=product[:])
+                return products, None
+            head_sumsq = small.tile([P, len(group), HEADS], F32)
+            for i, product in enumerate(products):
+                head_squares = stage.tile([P, HEADS, HEAD], BF16)
+                for h in range(HEADS):
                     nc.scalar.activation(
-                        out=head_rms[:], in_=head_sumsq[:], func=ACT.Sqrt, scale=1.0 / HEAD, bias=eps[:]
+                        out=head_squares[:, h, :],
+                        in_=product[:, h, :],
+                        func=ACT.Square,
+                        accum_out=head_sumsq[:, i, h : h + 1],
                     )
-                    head_rinv = small.tile([P, HEADS], F32)
-                    nc.vector.reciprocal(out=head_rinv[:], in_=head_rms[:])
+            head_rms = small.tile([P, len(group), HEADS], F32)
+            nc.scalar.activation(out=head_rms[:], in_=head_sumsq[:], func=ACT.Sqrt, scale=1.0 / HEAD, bias=eps[:])
+            head_rinv = small.tile([P, len(group), HEADS], F32)
+            nc.vector.reciprocal(out=head_rinv[:], in_=head_rms[:])
+            return products, head_rinv
+
+        def rope_and_store(group, m, products, head_rinv):
+            norm = group[0][5]
+            for i, (block, product) in enumerate(zip(group, products)):
+                result = finished[block[2]]
+                if norm is not None:
                     terms = stage.tile([P, HEADS, 2, HEAD], F32, bufs=6)
                     for h in range(HEADS):
                         nc.vector.scalar_tensor_tensor(
                             out=terms[:, h],
                             in0=product[:, h, :].unsqueeze(1).to_broadcast([P, 2, HEAD]),
-                            scalar=head_rinv[:, h : h + 1],
+                            scalar=head_rinv[:, i, h : h + 1],
                             in1=rope[norm][:, m],
                             op0=ALU.mult,
                             op1=ALU.mult,
                         )
-                    nc.vector.tensor_tensor(
-                        out=finished[:, :, m, :].rearrange("p h (s j) -> p h s j", s=2),
+                    adder = nc.vector if block[2] == last_rope_col else nc.gpsimd
+                    adder.tensor_tensor(
+                        out=result[:, :, m, :].rearrange("p h (s j) -> p h s j", s=2),
                         in0=terms[:, :, 0, :].rearrange("p h (s j) -> p h s j", s=2),
                         in1=terms[:, :, 1, :].rearrange("p h (s j) -> p h s j", s=2)[:, :, ::-1, :],
                         op=ALU.add,
                     )
-            nc.sync.dma_start(
-                out=out.rearrange("b h (p m) d -> p (b h) (m d)", m=TILES)[:, first_head : first_head + HEADS, :],
-                in_=finished[:].rearrange("p h m d -> p h (m d)"),
-            )
+                if m == TILES - 1:
+                    out, first_head = block[3], block[4]
+                    queue = nc.scalar if norm is None else nc.sync
+                    queue.dma_start(
+                        out=out.rearrange("b h (p m) d -> p (b h) (m d)", m=TILES)[
+                            :, first_head : first_head + HEADS, :
+                        ],
+                        in_=result[:].rearrange("p h m d -> p h (m d)"),
+                    )
+
+        steps = []
+        for m in range(TILES):
+            steps.append((blocks[:PAIR], m))
+        for block in blocks[PAIR:]:
+            for m in range(TILES):
+                steps.append(([block], m))
+        held = None
+        for group, m in steps:
+            products, head_rinv = products_and_norms(group, m)
+            if held is not None:
+                rope_and_store(*held)
+            held = (group, m, products, head_rinv)
+        rope_and_store(*held)

@@ -67,11 +67,25 @@ def tile_rawkvinjector_pa_kernel(
 
         x_all = keep.tile([P, TILES, D_MODEL], BF16)
         x_rows = hidden_states.rearrange("b (p m) k -> p (b m) k", m=TILES)
-        for m in range(TILES):
-            nc.sync.dma_start(out=x_all[:, m, :], in_=x_rows[:, m, :])
+        norm_rows = keep.tile([P, 2 * HEAD], BF16)
+        nc.vector.memset(norm_rows[:].bitcast(I32), 0)
+        ln_w = keep.tile([P, PASSES, PACK], BF16)
+        nc.sync.dma_start(out=x_all[:, 0, :], in_=x_rows[:, 0, :])
+        nc.sync.dma_start(out=x_all[:, 1, :], in_=x_rows[:, 1, :])
+        nc.sync.dma_start(out=norm_rows[0:1, :HEAD], in_=q_norm_w.unsqueeze(0))
+        nc.sync.dma_start(out=norm_rows[0:1, HEAD:], in_=k_norm_w.unsqueeze(0))
+        nc.sync.dma_start(out=x_all[:, 2, :], in_=x_rows[:, 2, :])
+        nc.sync.dma_start(out=ln_w[:], in_=ln1_w.rearrange("(g p t) -> p g t", p=P, t=PACK))
 
         w_planes = keep.tile([P, N_ALL], U8, align_bytes=64)
         nc.vector.memset(w_planes[:].bitcast(I32), 0)
+
+        cos_rows = keep.tile([P, TILES, HEAD], BF16)
+        nc.gpsimd.dma_start(out=cos_rows[:], in_=cos.rearrange("(p m) d -> p m d", m=TILES))
+        sin_rows = keep.tile([P, TILES, HEAD], BF16)
+        nc.gpsimd.dma_start(out=sin_rows[:], in_=sin.rearrange("(p m) d -> p m d", m=TILES))
+
+        blocks = []
         plane_col = 0
         for words, scales, out, norm in projections:
             n_cols = scales.shape[2]
@@ -82,22 +96,6 @@ def tile_rawkvinjector_pa_kernel(
                     ].bitcast(I32),
                     in_=scales[:, 4 * quad : 4 * quad + 4, :].bitcast(I32),
                 )
-            plane_col += n_cols
-
-        ln_w = keep.tile([P, PASSES, PACK], BF16)
-        nc.scalar.dma_start(out=ln_w[:], in_=ln1_w.rearrange("(g p t) -> p g t", p=P, t=PACK))
-        cos_rows = keep.tile([P, TILES, HEAD], BF16)
-        nc.scalar.dma_start(out=cos_rows[:], in_=cos.rearrange("(p m) d -> p m d", m=TILES))
-        sin_rows = keep.tile([P, TILES, HEAD], BF16)
-        nc.scalar.dma_start(out=sin_rows[:], in_=sin.rearrange("(p m) d -> p m d", m=TILES))
-        norm_rows = keep.tile([P, 2 * HEAD], BF16)
-        nc.vector.memset(norm_rows[:].bitcast(I32), 0)
-        nc.scalar.dma_start(out=norm_rows[0:1, :HEAD], in_=q_norm_w.unsqueeze(0))
-        nc.scalar.dma_start(out=norm_rows[0:1, HEAD:], in_=k_norm_w.unsqueeze(0))
-
-        blocks = []
-        plane_col = 0
-        for words, scales, out, norm in projections:
             for n0 in range(0, words.shape[2], PAIR * N_BLOCK):
                 w_words = keep.tile([P, PASSES, PAIR * N_BLOCK], U32, name="w_words%d" % plane_col, align_bytes=64)
                 for g in range(PASSES):
@@ -119,6 +117,44 @@ def tile_rawkvinjector_pa_kernel(
         make_identity(nc, identity[:])
         ones = keep.tile([P, P], BF16)
         nc.vector.memset(ones[:], 1.0)
+
+        x_sumsq = keep.tile([P, TILES], F32)
+        x_rms = keep.tile([P, TILES], F32)
+        x_rinv = keep.tile([P, TILES], F32)
+        v_sumsq = keep.tile([P, 1], F32)
+        v_share = keep.tile([P, 1], F32)
+
+        def token_norms(m):
+            s_cols = D_MODEL // 2 if m == 0 else D_MODEL
+            squares = stage.tile([P, D_MODEL], BF16)
+            nc.scalar.activation(
+                out=squares[:, :s_cols], in_=x_all[:, m, :s_cols], func=ACT.Square, accum_out=x_sumsq[:, m : m + 1]
+            )
+            if m == 0:
+                v_squares = stage.tile([P, D_MODEL // 2], BF16)
+                nc.vector.scalar_tensor_tensor(
+                    out=v_squares[:],
+                    in0=x_all[:, m, s_cols:],
+                    scalar=1.0,
+                    in1=x_all[:, m, s_cols:],
+                    op0=ALU.mult,
+                    op1=ALU.mult,
+                    accum_out=v_sumsq[:],
+                )
+                nc.vector.tensor_scalar(
+                    out=v_share[:], in0=v_sumsq[:], scalar1=1.0 / D_MODEL, scalar2=EPS, op0=ALU.mult, op1=ALU.add
+                )
+            nc.scalar.activation(
+                out=x_rms[:, m : m + 1],
+                in_=x_sumsq[:, m : m + 1],
+                func=ACT.Sqrt,
+                scale=1.0 / D_MODEL,
+                bias=v_share[:] if m == 0 else eps[:],
+            )
+            nc.vector.reciprocal(out=x_rinv[:, m : m + 1], in_=x_rms[:, m : m + 1])
+
+        for m in range(TILES):
+            token_norms(m)
 
         norm_w = turned.tile([P, 2, HEAD], F32, tag="flipped")
         nc.tensor.matmul(
@@ -149,9 +185,6 @@ def tile_rawkvinjector_pa_kernel(
 
         h_words = keep.tile([P, TILES, PASSES, P], U32, align_bytes=64)
         h_planes = keep.tile([P, TILES, PASSES, P], U8, align_bytes=64)
-        x_sumsq = keep.tile([P, TILES], F32)
-        x_rms = keep.tile([P, TILES], F32)
-        x_rinv = keep.tile([P, TILES], F32)
         def quantise(chunk):
             m, g, grouped = chunk
             nc.vector.quantize_mx(
@@ -162,22 +195,10 @@ def tile_rawkvinjector_pa_kernel(
 
         copied = None
         for m in range(TILES):
-            squares = stage.tile([P, D_MODEL], BF16)
-            nc.scalar.activation(
-                out=squares[:], in_=x_all[:, m, :], func=ACT.Square, accum_out=x_sumsq[:, m : m + 1]
-            )
-            nc.scalar.activation(
-                out=x_rms[:, m : m + 1],
-                in_=x_sumsq[:, m : m + 1],
-                func=ACT.Sqrt,
-                scale=1.0 / D_MODEL,
-                bias=eps[:],
-            )
-            nc.vector.reciprocal(out=x_rinv[:, m : m + 1], in_=x_rms[:, m : m + 1])
             for g in range(PASSES):
                 scaled = stage.tile([P, PACK, P], F32, bufs=4)
                 sorted_x = x_all[:, m, g * K_PASS : (g + 1) * K_PASS].rearrange("r (p t) -> r t p", t=PACK)
-                if g < PASSES - 1:
+                if g < PASSES - m:
                     nc.gpsimd.tensor_scalar(
                         out=scaled[:],
                         in0=sorted_x,

@@ -67,15 +67,14 @@ def tile_rawkvinjector_pa_kernel(
 
         x_all = keep.tile([P, TILES, D_MODEL], BF16)
         x_rows = hidden_states.rearrange("b (p m) k -> p (b m) k", m=TILES)
-        norm_rows = keep.tile([P, 2 * HEAD], BF16)
-        nc.vector.memset(norm_rows[:].bitcast(I32), 0)
-        ln_w = keep.tile([P, PASSES, PACK], BF16)
+        weight_rows = keep.tile([P, D_MODEL + 2 * HEAD], BF16)
+        nc.vector.memset(weight_rows[:].bitcast(I32), 0)
         nc.sync.dma_start(out=x_all[:, 0, :], in_=x_rows[:, 0, :])
+        nc.sync.dma_start(out=weight_rows[0:1, :D_MODEL], in_=ln1_w.unsqueeze(0))
         nc.sync.dma_start(out=x_all[:, 1, :], in_=x_rows[:, 1, :])
-        nc.sync.dma_start(out=norm_rows[0:1, :HEAD], in_=q_norm_w.unsqueeze(0))
-        nc.sync.dma_start(out=norm_rows[0:1, HEAD:], in_=k_norm_w.unsqueeze(0))
         nc.sync.dma_start(out=x_all[:, 2, :], in_=x_rows[:, 2, :])
-        nc.sync.dma_start(out=ln_w[:], in_=ln1_w.rearrange("(g p t) -> p g t", p=P, t=PACK))
+        nc.sync.dma_start(out=weight_rows[0:1, D_MODEL : D_MODEL + HEAD], in_=q_norm_w.unsqueeze(0))
+        nc.sync.dma_start(out=weight_rows[0:1, D_MODEL + HEAD :], in_=k_norm_w.unsqueeze(0))
 
         w_planes = keep.tile([P, N_ALL], U8, align_bytes=64)
         nc.vector.memset(w_planes[:].bitcast(I32), 0)
@@ -117,6 +116,17 @@ def tile_rawkvinjector_pa_kernel(
         make_identity(nc, identity[:])
         ones = keep.tile([P, P], BF16)
         nc.vector.memset(ones[:], 1.0)
+        ln_bank = []
+        for g in range(PASSES):
+            spread = sums.tile([P, K_PASS], F32, tag="product")
+            nc.tensor.matmul(
+                out=spread[:], lhsT=ones[:], rhs=weight_rows[:, g * K_PASS : (g + 1) * K_PASS], start=True, stop=True
+            )
+            ln_bank.append(spread)
+        norm_bank = turned.tile([P, 2 * HEAD], F32, tag="flipped")
+        nc.tensor.matmul(out=norm_bank[:], lhsT=ones[:], rhs=weight_rows[:, D_MODEL:], start=True, stop=True)
+        norm_w = keep.tile([P, 2, HEAD], F32)
+        nc.scalar.copy(out=norm_w[:].rearrange("p n d -> p (n d)"), in_=norm_bank[:])
 
         x_sumsq = keep.tile([P, TILES], F32)
         x_rms = keep.tile([P, TILES], F32)
@@ -156,73 +166,65 @@ def tile_rawkvinjector_pa_kernel(
         for m in range(TILES):
             token_norms(m)
 
-        norm_w = turned.tile([P, 2, HEAD], F32, tag="flipped")
-        nc.tensor.matmul(
-            out=norm_w[:].rearrange("p n d -> p (n d)"), lhsT=ones[:], rhs=norm_rows[:], start=True, stop=True
-        )
-        rope = []
-        for norm in range(2):
-            table = keep.tile([P, TILES, 2, HEAD], F32, name="rope%d" % norm)
-            w_all = norm_w[:, norm, :].unsqueeze(1)
-            nc.vector.tensor_tensor(
-                out=table[:, :, 0, :], in0=cos_rows[:], in1=w_all.to_broadcast([P, TILES, HEAD]), op=ALU.mult
-            )
-            nc.vector.tensor_tensor(
-                out=table[:, :, 1, :HALF],
-                in0=sin_rows[:, :, HALF:],
-                in1=w_all[:, :, :HALF].to_broadcast([P, TILES, HALF]),
-                op=ALU.mult,
-            )
-            nc.vector.scalar_tensor_tensor(
-                out=table[:, :, 1, HALF:],
-                in0=sin_rows[:, :, :HALF],
-                scalar=-1.0,
-                in1=w_all[:, :, HALF:].to_broadcast([P, TILES, HALF]),
-                op0=ALU.mult,
-                op1=ALU.mult,
-            )
-            rope.append(table)
-
         h_words = keep.tile([P, TILES, PASSES, P], U32, align_bytes=64)
         h_planes = keep.tile([P, TILES, PASSES, P], U8, align_bytes=64)
+
         def quantise(chunk):
             m, g, grouped = chunk
             nc.vector.quantize_mx(
                 out=h_words[:, m, g, :].bitcast(FP8X4),
                 scales=h_planes[:, m, g, :],
-                in_=grouped[:].rearrange("p r t -> p (r t)"),
+                in_=grouped[:].rearrange("p r u -> p (r u)").bitcast(BF16),
             )
 
         copied = None
         for m in range(TILES):
+            h_rows = stage.tile([P, D_MODEL], BF16, bufs=TILES)
             for g in range(PASSES):
-                scaled = stage.tile([P, PACK, P], F32, bufs=4)
-                sorted_x = x_all[:, m, g * K_PASS : (g + 1) * K_PASS].rearrange("r (p t) -> r t p", t=PACK)
-                if g < PASSES - m:
-                    nc.gpsimd.tensor_scalar(
-                        out=scaled[:],
-                        in0=sorted_x,
-                        scalar1=x_rinv[:, m : m + 1],
-                        scalar2=0.0,
-                        op0=ALU.mult,
-                        op1=ALU.add,
-                    )
-                else:
-                    nc.scalar.activation(out=scaled[:], in_=sorted_x, func=ACT.Copy, scale=x_rinv[:, m : m + 1])
-                flipped = turned.tile([P, PACK, P], F32)
-                for t in range(PACK):
-                    nc.tensor.transpose(flipped[:, t, :], scaled[:, t, :], identity[:])
-                grouped = stage.tile([P, P, PACK], BF16, bufs=4, align_bytes=64)
-                nc.vector.tensor_tensor(
-                    out=grouped[:],
-                    in0=flipped[:].rearrange("p t r -> p r t"),
-                    in1=ln_w[:, g, :].unsqueeze(1).to_broadcast([P, P, PACK]),
-                    op=ALU.mult,
+                k_range = slice(g * K_PASS, (g + 1) * K_PASS)
+                nc.vector.scalar_tensor_tensor(
+                    out=h_rows[:, k_range],
+                    in0=x_all[:, m, k_range],
+                    scalar=x_rinv[:, m : m + 1],
+                    in1=ln_bank[g][:],
+                    op0=ALU.mult,
+                    op1=ALU.mult,
                 )
+                pairs = h_rows[:, k_range].bitcast(F32)
+                flipped = turned.tile([P, 2, P], F32)
+                for u in range(2):
+                    nc.tensor.transpose(flipped[:, u, :], pairs[:, u : K_PASS // 2 : 2], identity[:])
+                grouped = stage.tile([P, P, 2], F32, bufs=4, align_bytes=64)
+                nc.scalar.copy(out=grouped[:], in_=flipped[:].rearrange("p u r -> p r u"))
                 if copied is not None:
                     quantise(copied)
                 copied = (m, g, grouped)
         quantise(copied)
+
+        minus_w = keep.tile([P, 2, HALF], F32)
+        nc.gpsimd.tensor_scalar(
+            out=minus_w[:], in0=norm_w[:, :, HALF:], scalar1=-1.0, scalar2=0.0, op0=ALU.mult, op1=ALU.add
+        )
+        rope = []
+        for norm in range(2):
+            table = keep.tile([P, TILES, 2, HEAD], F32, name="rope%d" % norm)
+            w_all = norm_w[:, norm, :].unsqueeze(1)
+            nc.gpsimd.tensor_tensor(
+                out=table[:, :, 0, :], in0=cos_rows[:], in1=w_all.to_broadcast([P, TILES, HEAD]), op=ALU.mult
+            )
+            nc.gpsimd.tensor_tensor(
+                out=table[:, :, 1, :HALF],
+                in0=sin_rows[:, :, HALF:],
+                in1=w_all[:, :, :HALF].to_broadcast([P, TILES, HALF]),
+                op=ALU.mult,
+            )
+            nc.gpsimd.tensor_tensor(
+                out=table[:, :, 1, HALF:],
+                in0=sin_rows[:, :, :HALF],
+                in1=minus_w[:, norm, :].unsqueeze(1).to_broadcast([P, TILES, HALF]),
+                op=ALU.mult,
+            )
+            rope.append(table)
 
         finished = {}
         last_rope_col = max(block[2] for block in blocks if block[5] is not None)

@@ -227,7 +227,6 @@ def tile_rawkvinjector_pa_kernel(
             rope.append(table)
 
         finished = {}
-        last_rope_col = max(block[2] for block in blocks if block[5] is not None)
 
         def products_and_norms(group, m):
             norm = group[0][5]
@@ -285,8 +284,7 @@ def tile_rawkvinjector_pa_kernel(
                             op0=ALU.mult,
                             op1=ALU.mult,
                         )
-                    adder = nc.vector if block[2] == last_rope_col else nc.gpsimd
-                    adder.tensor_tensor(
+                    nc.gpsimd.tensor_tensor(
                         out=result[:, :, m, :].rearrange("p h (s j) -> p h s j", s=2),
                         in0=terms[:, :, 0, :].rearrange("p h (s j) -> p h s j", s=2),
                         in1=terms[:, :, 1, :].rearrange("p h (s j) -> p h s j", s=2)[:, :, ::-1, :],

@@ -170,35 +170,38 @@ def tile_rawkvinjector_pa_kernel(
         h_planes = keep.tile([P, TILES, PASSES, P], U8, align_bytes=64)
 
         def quantise(chunk):
-            m, g, grouped = chunk
+            m, first, grouped = chunk
             nc.vector.quantize_mx(
-                out=h_words[:, m, g, :].bitcast(FP8X4),
-                scales=h_planes[:, m, g, :],
-                in_=grouped[:].rearrange("p r u -> p (r u)").bitcast(BF16),
+                out=h_words[:, m, first : first + 2, :].rearrange("p g c -> p (g c)").bitcast(FP8X4),
+                scales=h_planes[:, m, first : first + 2, :].rearrange("p g c -> p (g c)"),
+                in_=grouped[:].rearrange("p i r u -> p (i r u)").bitcast(BF16),
             )
 
         copied = None
         for m in range(TILES):
             h_rows = stage.tile([P, D_MODEL], BF16, bufs=TILES)
-            for g in range(PASSES):
-                k_range = slice(g * K_PASS, (g + 1) * K_PASS)
-                nc.vector.scalar_tensor_tensor(
-                    out=h_rows[:, k_range],
-                    in0=x_all[:, m, k_range],
-                    scalar=x_rinv[:, m : m + 1],
-                    in1=ln_bank[g][:],
-                    op0=ALU.mult,
-                    op1=ALU.mult,
-                )
-                pairs = h_rows[:, k_range].bitcast(F32)
-                flipped = turned.tile([P, 2, P], F32)
-                for u in range(2):
-                    nc.tensor.transpose(flipped[:, u, :], pairs[:, u : K_PASS // 2 : 2], identity[:])
-                grouped = stage.tile([P, P, 2], F32, bufs=4, align_bytes=64)
-                nc.scalar.copy(out=grouped[:], in_=flipped[:].rearrange("p u r -> p r u"))
+            for first in range(0, PASSES, 2):
+                for g in (first, first + 1):
+                    k_range = slice(g * K_PASS, (g + 1) * K_PASS)
+                    nc.vector.scalar_tensor_tensor(
+                        out=h_rows[:, k_range],
+                        in0=x_all[:, m, k_range],
+                        scalar=x_rinv[:, m : m + 1],
+                        in1=ln_bank[g][:],
+                        op0=ALU.mult,
+                        op1=ALU.mult,
+                    )
+                flipped = turned.tile([P, 2, 2, P], F32)
+                for i in range(2):
+                    g = first + i
+                    pairs = h_rows[:, g * K_PASS : (g + 1) * K_PASS].bitcast(F32)
+                    for u in range(2):
+                        nc.tensor.transpose(flipped[:, i, u, :], pairs[:, u : K_PASS // 2 : 2], identity[:])
+                grouped = stage.tile([P, 2, P, 2], F32, bufs=4, align_bytes=64)
+                nc.scalar.copy(out=grouped[:], in_=flipped[:].rearrange("p i u r -> p i r u"))
                 if copied is not None:
                     quantise(copied)
-                copied = (m, g, grouped)
+                copied = (m, first, grouped)
         quantise(copied)
 
         minus_w = keep.tile([P, 2, HALF], F32)

@@ -169,39 +169,44 @@ def tile_rawkvinjector_pa_kernel(
         h_words = keep.tile([P, TILES, PASSES, P], U32, align_bytes=64)
         h_planes = keep.tile([P, TILES, PASSES, P], U8, align_bytes=64)
 
-        def quantise(chunk):
-            m, first, grouped = chunk
+        def quantise(tile):
+            m, grouped = tile
             nc.vector.quantize_mx(
-                out=h_words[:, m, first : first + 2, :].rearrange("p g c -> p (g c)").bitcast(FP8X4),
-                scales=h_planes[:, m, first : first + 2, :].rearrange("p g c -> p (g c)"),
-                in_=grouped[:].rearrange("p i r u -> p (i r u)").bitcast(BF16),
+                out=h_words[:, m].rearrange("p g c -> p (g c)").bitcast(FP8X4),
+                scales=h_planes[:, m].rearrange("p g c -> p (g c)"),
+                in_=grouped[:].rearrange("p g r u -> p (g r u)").bitcast(BF16),
             )
 
         copied = None
         for m in range(TILES):
             h_rows = stage.tile([P, D_MODEL], BF16, bufs=TILES)
+            for g in range(PASSES):
+                k_range = slice(g * K_PASS, (g + 1) * K_PASS)
+                nc.vector.scalar_tensor_tensor(
+                    out=h_rows[:, k_range],
+                    in0=x_all[:, m, k_range],
+                    scalar=x_rinv[:, m : m + 1],
+                    in1=ln_bank[g][:],
+                    op0=ALU.mult,
+                    op1=ALU.mult,
+                )
+            if copied is not None:
+                quantise(copied)
+            banks = []
             for first in range(0, PASSES, 2):
-                for g in (first, first + 1):
-                    k_range = slice(g * K_PASS, (g + 1) * K_PASS)
-                    nc.vector.scalar_tensor_tensor(
-                        out=h_rows[:, k_range],
-                        in0=x_all[:, m, k_range],
-                        scalar=x_rinv[:, m : m + 1],
-                        in1=ln_bank[g][:],
-                        op0=ALU.mult,
-                        op1=ALU.mult,
-                    )
                 flipped = turned.tile([P, 2, 2, P], F32)
+                banks.append(flipped)
                 for i in range(2):
                     g = first + i
                     pairs = h_rows[:, g * K_PASS : (g + 1) * K_PASS].bitcast(F32)
                     for u in range(2):
                         nc.tensor.transpose(flipped[:, i, u, :], pairs[:, u : K_PASS // 2 : 2], identity[:])
-                grouped = stage.tile([P, 2, P, 2], F32, bufs=4, align_bytes=64)
-                nc.scalar.copy(out=grouped[:], in_=flipped[:].rearrange("p i u r -> p i r u"))
-                if copied is not None:
-                    quantise(copied)
-                copied = (m, first, grouped)
+            grouped = stage.tile([P, PASSES, P, 2], F32, bufs=TILES, align_bytes=64)
+            for half, flipped in enumerate(banks):
+                nc.scalar.copy(
+                    out=grouped[:, 2 * half : 2 * half + 2], in_=flipped[:].rearrange("p i u r -> p i r u")
+                )
+            copied = (m, grouped)
         quantise(copied)
 
         minus_w = keep.tile([P, 2, HALF], F32)

@@ -235,12 +235,17 @@ def tile_rawkvinjector_pa_kernel(
             rope.append(table)
 
         finished = {}
+        opened = []
 
         def products_and_norms(group, m):
             norm = group[0][5]
             products = []
             for block in group:
-                product = sums.tile([P, HEADS, HEAD], F32)
+                if len(opened) >= TILES * PAIR and len(opened) % 4 == 1:
+                    product = turned.tile([P, HEADS, HEAD], F32, tag="flipped")
+                else:
+                    product = sums.tile([P, HEADS, HEAD], F32)
+                opened.append(product)
                 products.append(product)
                 if m == 0:
                     result = results.tile([P, HEADS, TILES, HEAD], F32)

@@ -117,11 +117,16 @@ def tile_rawkvinjector_pa_kernel(
         ones = keep.tile([P, P], BF16)
         nc.vector.memset(ones[:], 1.0)
         ln_bank = []
-        for g in range(PASSES):
-            spread = sums.tile([P, K_PASS], F32, tag="product")
-            nc.tensor.matmul(
-                out=spread[:], lhsT=ones[:], rhs=weight_rows[:, g * K_PASS : (g + 1) * K_PASS], start=True, stop=True
-            )
+        for first in range(0, PASSES, 2):
+            spread = sums.tile([P, 2 * K_PASS], BF16, tag="product")
+            for i in range(2):
+                nc.tensor.matmul(
+                    out=spread[:, i * K_PASS : (i + 1) * K_PASS],
+                    lhsT=ones[:],
+                    rhs=weight_rows[:, (first + i) * K_PASS : (first + i + 1) * K_PASS],
+                    start=True,
+                    stop=True,
+                )
             ln_bank.append(spread)
         norm_bank = turned.tile([P, 2 * HEAD], F32, tag="flipped")
         nc.tensor.matmul(out=norm_bank[:], lhsT=ones[:], rhs=weight_rows[:, D_MODEL:], start=True, stop=True)
@@ -180,13 +185,13 @@ def tile_rawkvinjector_pa_kernel(
         copied = None
         for m in range(TILES):
             h_rows = stage.tile([P, D_MODEL], BF16, bufs=TILES)
-            for g in range(PASSES):
-                k_range = slice(g * K_PASS, (g + 1) * K_PASS)
+            for half in range(2):
+                k_range = slice(half * 2 * K_PASS, (half + 1) * 2 * K_PASS)
                 nc.vector.scalar_tensor_tensor(
                     out=h_rows[:, k_range],
                     in0=x_all[:, m, k_range],
                     scalar=x_rinv[:, m : m + 1],
-                    in1=ln_bank[g][:],
+                    in1=ln_bank[half][:],
                     op0=ALU.mult,
                     op1=ALU.mult,
                 )

@@ -184,28 +184,30 @@ def tile_rawkvinjector_pa_kernel(
 
         copied = None
         for m in range(TILES):
-            h_rows = stage.tile([P, D_MODEL], BF16, bufs=TILES)
+            h_sorted = stage.tile([P, 2, 2, 2 * P, 2], BF16, bufs=TILES)
             for half in range(2):
                 k_range = slice(half * 2 * K_PASS, (half + 1) * 2 * K_PASS)
-                nc.vector.scalar_tensor_tensor(
-                    out=h_rows[:, k_range],
-                    in0=x_all[:, m, k_range],
-                    scalar=x_rinv[:, m : m + 1],
-                    in1=ln_bank[half][:],
-                    op0=ALU.mult,
-                    op1=ALU.mult,
-                )
+                x_pairs = x_all[:, m, k_range].rearrange("r (q u e) -> r u q e", u=2, e=2)
+                ln_pairs = ln_bank[half][:].rearrange("r (q u e) -> r u q e", u=2, e=2)
+                for u in range(2):
+                    nc.vector.scalar_tensor_tensor(
+                        out=h_sorted[:, half, u],
+                        in0=x_pairs[:, u],
+                        scalar=x_rinv[:, m : m + 1],
+                        in1=ln_pairs[:, u],
+                        op0=ALU.mult,
+                        op1=ALU.mult,
+                    )
             if copied is not None:
                 quantise(copied)
             banks = []
-            for first in range(0, PASSES, 2):
+            for half in range(2):
                 flipped = turned.tile([P, 2, 2, P], F32)
                 banks.append(flipped)
                 for i in range(2):
-                    g = first + i
-                    pairs = h_rows[:, g * K_PASS : (g + 1) * K_PASS].bitcast(F32)
                     for u in range(2):
-                        nc.tensor.transpose(flipped[:, i, u, :], pairs[:, u : K_PASS // 2 : 2], identity[:])
+                        words = h_sorted[:, half, u, i * P : (i + 1) * P, :].rearrange("r q e -> r (q e)")
+                        nc.tensor.transpose(flipped[:, i, u, :], words.bitcast(F32), identity[:])
             grouped = stage.tile([P, PASSES, P, 2], F32, bufs=TILES, align_bytes=64)
             for half, flipped in enumerate(banks):
                 nc.scalar.copy(

@@ -64,24 +64,33 @@ def tile_rawkvinjector_pa_kernel(
         results = ctx.enter_context(tc.tile_pool(name="results", bufs=N_ALL // N_BLOCK))
         turned = ctx.enter_context(tc.psum_pool(name="turned", bufs=2))
         sums = ctx.enter_context(tc.psum_pool(name="sums", bufs=6))
+        ctx.enter_context(tc.manual_schedule())
 
         x_all = keep.tile([P, TILES, D_MODEL], BF16)
         x_rows = hidden_states.rearrange("b (p m) k -> p (b m) k", m=TILES)
         weight_rows = keep.tile([P, D_MODEL + 2 * HEAD], BF16)
-        nc.vector.memset(weight_rows[:].bitcast(I32), 0)
+        w_planes = keep.tile([P, N_ALL], U8, align_bytes=64)
+        eps = keep.tile([P, 1], F32)
+        ones = keep.tile([P, P], BF16)
+        table_warm = keep.tile([P, 1], F32)
+        identity = keep.tile([P, P], F32)
+        cos_rows = keep.tile([P, TILES, HEAD], BF16)
+        sin_rows = keep.tile([P, TILES, HEAD], BF16)
+
+        nc.gpsimd.memset(weight_rows[:].bitcast(I32), 0)
+        nc.vector.memset(eps[:], EPS)
+        nc.scalar.activation(out=table_warm[:], in_=eps[:], func=ACT.Sqrt)
+        nc.vector.memset(ones[:], 1.0)
+        nc.vector.memset(w_planes[:].bitcast(I32), 0)
+        make_identity(nc, identity[:])
+
         nc.sync.dma_start(out=x_all[:, 0, :], in_=x_rows[:, 0, :])
         nc.sync.dma_start(out=weight_rows[0:1, :D_MODEL], in_=ln1_w.unsqueeze(0))
         nc.sync.dma_start(out=x_all[:, 1, :], in_=x_rows[:, 1, :])
         nc.sync.dma_start(out=x_all[:, 2, :], in_=x_rows[:, 2, :])
         nc.sync.dma_start(out=weight_rows[0:1, D_MODEL : D_MODEL + HEAD], in_=q_norm_w.unsqueeze(0))
         nc.sync.dma_start(out=weight_rows[0:1, D_MODEL + HEAD :], in_=k_norm_w.unsqueeze(0))
-
-        w_planes = keep.tile([P, N_ALL], U8, align_bytes=64)
-        nc.vector.memset(w_planes[:].bitcast(I32), 0)
-
-        cos_rows = keep.tile([P, TILES, HEAD], BF16)
         nc.gpsimd.dma_start(out=cos_rows[:], in_=cos.rearrange("(p m) d -> p m d", m=TILES))
-        sin_rows = keep.tile([P, TILES, HEAD], BF16)
         nc.gpsimd.dma_start(out=sin_rows[:], in_=sin.rearrange("(p m) d -> p m d", m=TILES))
 
         blocks = []
@@ -108,14 +117,6 @@ def tile_rawkvinjector_pa_kernel(
                     blocks.append((w_words, i * N_BLOCK, plane_col, out, (n0 + i * N_BLOCK) // HEAD, norm))
                     plane_col += N_BLOCK
 
-        eps = keep.tile([P, 1], F32)
-        nc.vector.memset(eps[:], EPS)
-        table_warm = keep.tile([P, 1], F32)
-        nc.scalar.activation(out=table_warm[:], in_=eps[:], func=ACT.Sqrt)
-        identity = keep.tile([P, P], F32)
-        make_identity(nc, identity[:])
-        ones = keep.tile([P, P], BF16)
-        nc.vector.memset(ones[:], 1.0)
         ln_bank = []
         for first in range(0, PASSES, 2):
             spread = sums.tile([P, 2 * K_PASS], BF16, tag="product")
@@ -128,18 +129,23 @@ def tile_rawkvinjector_pa_kernel(
                     stop=True,
                 )
             ln_bank.append(spread)
-        norm_bank = turned.tile([P, 2 * HEAD], F32, tag="flipped")
+        norm_bank = sums.tile([P, 2 * HEAD], F32, tag="product")
         nc.tensor.matmul(out=norm_bank[:], lhsT=ones[:], rhs=weight_rows[:, D_MODEL:], start=True, stop=True)
         norm_w = keep.tile([P, 2, HEAD], F32)
-        nc.scalar.copy(out=norm_w[:].rearrange("p n d -> p (n d)"), in_=norm_bank[:])
 
         x_sumsq = keep.tile([P, TILES], F32)
         x_rms = keep.tile([P, TILES], F32)
         x_rinv = keep.tile([P, TILES], F32)
         v_sumsq = keep.tile([P, 1], F32)
         v_share = keep.tile([P, 1], F32)
+        h_words = keep.tile([P, TILES, PASSES, P], U32, align_bytes=64)
+        h_planes = keep.tile([P, TILES, PASSES, P], U8, align_bytes=64)
+        grouped = []
+        for m in range(TILES):
+            grouped_m = keep.tile([P, PASSES, P, 2], F32, name="grouped%d" % m, align_bytes=64)
+            grouped.append(grouped_m)
 
-        def token_norms(m):
+        def token_rms(m):
             s_cols = D_MODEL // 2 if m == 0 else D_MODEL
             squares = stage.tile([P, D_MODEL], BF16)
             nc.scalar.activation(
@@ -166,55 +172,159 @@ def tile_rawkvinjector_pa_kernel(
                 scale=1.0 / D_MODEL,
                 bias=v_share[:] if m == 0 else eps[:],
             )
+
+        def token_rinv(m):
             nc.vector.reciprocal(out=x_rinv[:, m : m + 1], in_=x_rms[:, m : m + 1])
 
-        for m in range(TILES):
-            token_norms(m)
+        def normalise(m, half):
+            h_sorted = stage.tile([P, 2, 2 * P, 2], BF16, bufs=4)
+            k_range = slice(half * 2 * K_PASS, (half + 1) * 2 * K_PASS)
+            x_pairs = x_all[:, m, k_range].rearrange("r (q u e) -> r u q e", u=2, e=2)
+            ln_pairs = ln_bank[half][:].rearrange("r (q u e) -> r u q e", u=2, e=2)
+            for u in range(2):
+                nc.vector.scalar_tensor_tensor(
+                    out=h_sorted[:, u],
+                    in0=x_pairs[:, u],
+                    scalar=x_rinv[:, m : m + 1],
+                    in1=ln_pairs[:, u],
+                    op0=ALU.mult,
+                    op1=ALU.mult,
+                )
+            return h_sorted
 
-        h_words = keep.tile([P, TILES, PASSES, P], U32, align_bytes=64)
-        h_planes = keep.tile([P, TILES, PASSES, P], U8, align_bytes=64)
+        def flip(h_sorted):
+            flipped = turned.tile([P, 2, 2, P], F32)
+            for i in range(2):
+                for u in range(2):
+                    words = h_sorted[:, u, i * P : (i + 1) * P, :].rearrange("r q e -> r (q e)")
+                    nc.tensor.transpose(flipped[:, i, u, :], words.bitcast(F32), identity[:])
+            return flipped
 
-        def quantise(tile):
-            m, grouped = tile
-            nc.vector.quantize_mx(
-                out=h_words[:, m].rearrange("p g c -> p (g c)").bitcast(FP8X4),
-                scales=h_planes[:, m].rearrange("p g c -> p (g c)"),
-                in_=grouped[:].rearrange("p g r u -> p (g r u)").bitcast(BF16),
+        def group(m, half, flipped):
+            nc.scalar.copy(
+                out=grouped[m][:, 2 * half : 2 * half + 2], in_=flipped[:].rearrange("p i u r -> p i r u")
             )
 
-        copied = None
-        for m in range(TILES):
-            h_sorted = stage.tile([P, 2, 2, 2 * P, 2], BF16, bufs=TILES)
-            for half in range(2):
-                k_range = slice(half * 2 * K_PASS, (half + 1) * 2 * K_PASS)
-                x_pairs = x_all[:, m, k_range].rearrange("r (q u e) -> r u q e", u=2, e=2)
-                ln_pairs = ln_bank[half][:].rearrange("r (q u e) -> r u q e", u=2, e=2)
-                for u in range(2):
-                    nc.vector.scalar_tensor_tensor(
-                        out=h_sorted[:, half, u],
-                        in0=x_pairs[:, u],
-                        scalar=x_rinv[:, m : m + 1],
-                        in1=ln_pairs[:, u],
-                        op0=ALU.mult,
-                        op1=ALU.mult,
-                    )
-            if copied is not None:
-                quantise(copied)
-            banks = []
-            for half in range(2):
-                flipped = turned.tile([P, 2, 2, P], F32)
-                banks.append(flipped)
-                for i in range(2):
-                    for u in range(2):
-                        words = h_sorted[:, half, u, i * P : (i + 1) * P, :].rearrange("r q e -> r (q e)")
-                        nc.tensor.transpose(flipped[:, i, u, :], words.bitcast(F32), identity[:])
-            grouped = stage.tile([P, PASSES, P, 2], F32, bufs=TILES, align_bytes=64)
-            for half, flipped in enumerate(banks):
-                nc.scalar.copy(
-                    out=grouped[:, 2 * half : 2 * half + 2], in_=flipped[:].rearrange("p i u r -> p i r u")
+        def quantise(m, g0, g1):
+            nc.vector.quantize_mx(
+                out=h_words[:, m, g0:g1].rearrange("p g c -> p (g c)").bitcast(FP8X4),
+                scales=h_planes[:, m, g0:g1].rearrange("p g c -> p (g c)"),
+                in_=grouped[m][:, g0:g1].rearrange("p g r u -> p (g r u)").bitcast(BF16),
+            )
+
+        finished = {}
+        opened = []
+
+        def open_bank(block, m):
+            if len(opened) >= TILES * PAIR and len(opened) % 4 == 1:
+                product = turned.tile([P, HEADS, HEAD], F32, tag="flipped")
+            else:
+                product = sums.tile([P, HEADS, HEAD], F32)
+            opened.append(product)
+            if m == 0:
+                result = results.tile([P, HEADS, TILES, HEAD], F32)
+                finished[block[2]] = result
+            return product
+
+        def passes(block, m, product, g0, g1):
+            w_words, words_col, plane_col = block[0], block[1], block[2]
+            for g in range(g0, g1):
+                nc.tensor.matmul_mx(
+                    out=product[:].rearrange("p h d -> p (h d)"),
+                    lhsT=h_words[:, m, g, :].bitcast(FP8X4),
+                    lhsT_scale=h_planes[:, m, g, :],
+                    rhs=w_words[:, g, words_col : words_col + N_BLOCK].bitcast(FP8X4),
+                    rhs_scale=w_planes[4 * g : P, plane_col : plane_col + N_BLOCK],
+                    start=(g == 0),
+                    stop=(g == PASSES - 1),
                 )
-            copied = (m, grouped)
-        quantise(copied)
+
+        def head_rms(product):
+            head_sumsq = small.tile([P, HEADS], F32)
+            head_squares = stage.tile([P, HEADS, HEAD], BF16)
+            for h in range(HEADS):
+                nc.scalar.activation(
+                    out=head_squares[:, h, :],
+                    in_=product[:, h, :],
+                    func=ACT.Square,
+                    accum_out=head_sumsq[:, h : h + 1],
+                )
+            rms = small.tile([P, HEADS], F32)
+            nc.scalar.activation(out=rms[:], in_=head_sumsq[:], func=ACT.Sqrt, scale=1.0 / HEAD, bias=eps[:])
+            return rms
+
+        def head_rinv(rms):
+            rinv = small.tile([P, HEADS], F32)
+            nc.vector.reciprocal(out=rinv[:], in_=rms[:])
+            return rinv
+
+        def rope_heads(block, m, product, rinv, terms, h0, h1):
+            for h in range(h0, h1):
+                nc.vector.scalar_tensor_tensor(
+                    out=terms[:, h],
+                    in0=product[:, h, :].unsqueeze(1).to_broadcast([P, 2, HEAD]),
+                    scalar=rinv[:, h : h + 1],
+                    in1=rope[block[5]][:, m],
+                    op0=ALU.mult,
+                    op1=ALU.mult,
+                )
+
+        def rope_sum(block, m, terms):
+            nc.gpsimd.tensor_tensor(
+                out=finished[block[2]][:, :, m, :].rearrange("p h (s j) -> p h s j", s=2),
+                in0=terms[:, :, 0, :].rearrange("p h (s j) -> p h s j", s=2),
+                in1=terms[:, :, 1, :].rearrange("p h (s j) -> p h s j", s=2)[:, :, ::-1, :],
+                op=ALU.add,
+            )
+
+        def store(block, queue):
+            out, first_head = block[3], block[4]
+            queue.dma_start(
+                out=out.rearrange("b h (p m) d -> p (b h) (m d)", m=TILES)[:, first_head : first_head + HEADS, :],
+                in_=finished[block[2]][:].rearrange("p h m d -> p h (m d)"),
+            )
+
+        b0, b1 = blocks[0], blocks[1]
+        token_rms(0)
+        token_rinv(0)
+        token_rms(1)
+        sorted00 = normalise(0, 0)
+        flipped00 = flip(sorted00)
+        sorted01 = normalise(0, 1)
+        flipped01 = flip(sorted01)
+        group(0, 0, flipped00)
+        token_rinv(1)
+        quantise(0, 0, 2)
+        token_rms(2)
+        p00 = open_bank(b0, 0)
+        p10 = open_bank(b1, 0)
+        passes(b0, 0, p00, 0, 1)
+        passes(b1, 0, p10, 0, 1)
+        passes(b0, 0, p00, 1, 2)
+        passes(b1, 0, p10, 1, 2)
+        sorted10 = normalise(1, 0)
+        flipped10 = flip(sorted10)
+        group(0, 1, flipped01)
+        sorted11 = normalise(1, 1)
+        flipped11 = flip(sorted11)
+        quantise(0, 2, 4)
+        token_rinv(2)
+        passes(b0, 0, p00, 2, 4)
+        passes(b1, 0, p10, 2, 4)
+        nc.scalar.copy(out=norm_w[:].rearrange("p n d -> p (n d)"), in_=norm_bank[:])
+        group(1, 0, flipped10)
+        group(1, 1, flipped11)
+        sorted20 = normalise(2, 0)
+        flipped20 = flip(sorted20)
+        quantise(1, 0, 4)
+        rms00 = head_rms(p00)
+        p01 = open_bank(b0, 1)
+        passes(b0, 1, p01, 0, 4)
+        sorted21 = normalise(2, 1)
+        flipped21 = flip(sorted21)
+        group(2, 0, flipped20)
+        rms10 = head_rms(p10)
+        group(2, 1, flipped21)
 
         minus_w = keep.tile([P, 2, HALF], F32)
         nc.gpsimd.tensor_scalar(
@@ -241,95 +351,43 @@ def tile_rawkvinjector_pa_kernel(
             )
             rope.append(table)
 
-        finished = {}
-        opened = []
+        rinv00 = head_rinv(rms00)
+        terms00 = stage.tile([P, HEADS, 2, HEAD], F32, bufs=6, tag="terms")
+        rope_heads(b0, 0, p00, rinv00, terms00, 0, HEADS)
+        rope_sum(b0, 0, terms00)
+        rinv10 = head_rinv(rms10)
+        quantise(2, 0, 4)
 
-        def products_and_norms(group, m):
-            norm = group[0][5]
-            products = []
-            for block in group:
-                if len(opened) >= TILES * PAIR and len(opened) % 4 == 1:
-                    product = turned.tile([P, HEADS, HEAD], F32, tag="flipped")
-                else:
-                    product = sums.tile([P, HEADS, HEAD], F32)
-                opened.append(product)
-                products.append(product)
-                if m == 0:
-                    result = results.tile([P, HEADS, TILES, HEAD], F32)
-                    finished[block[2]] = result
-            for g in range(PASSES):
-                for block, product in zip(group, products):
-                    w_words, words_col, plane_col = block[0], block[1], block[2]
-                    nc.tensor.matmul_mx(
-                        out=product[:].rearrange("p h d -> p (h d)"),
-                        lhsT=h_words[:, m, g, :].bitcast(FP8X4),
-                        lhsT_scale=h_planes[:, m, g, :],
-                        rhs=w_words[:, g, words_col : words_col + N_BLOCK].bitcast(FP8X4),
-                        rhs_scale=w_planes[4 * g : P, plane_col : plane_col + N_BLOCK],
-                        start=(g == 0),
-                        stop=(g == PASSES - 1),
-                    )
-            if norm is None:
-                for block, product in zip(group, products):
-                    nc.scalar.copy(out=finished[block[2]][:, :, m, :], in_=product[:])
-                return products, None
-            head_sumsq = small.tile([P, len(group), HEADS], F32)
-            for i, product in enumerate(products):
-                head_squares = stage.tile([P, HEADS, HEAD], BF16)
-                for h in range(HEADS):
-                    nc.scalar.activation(
-                        out=head_squares[:, h, :],
-                        in_=product[:, h, :],
-                        func=ACT.Square,
-                        accum_out=head_sumsq[:, i, h : h + 1],
-                    )
-            head_rms = small.tile([P, len(group), HEADS], F32)
-            nc.scalar.activation(out=head_rms[:], in_=head_sumsq[:], func=ACT.Sqrt, scale=1.0 / HEAD, bias=eps[:])
-            head_rinv = small.tile([P, len(group), HEADS], F32)
-            nc.vector.reciprocal(out=head_rinv[:], in_=head_rms[:])
-            return products, head_rinv
+        held = (b1, 0, p10, rinv10)
 
-        def rope_and_store(group, m, products, head_rinv):
-            norm = group[0][5]
-            for i, (block, product) in enumerate(zip(group, products)):
-                result = finished[block[2]]
-                if norm is not None:
-                    terms = stage.tile([P, HEADS, 2, HEAD], F32, bufs=6)
-                    for h in range(HEADS):
-                        nc.vector.scalar_tensor_tensor(
-                            out=terms[:, h],
-                            in0=product[:, h, :].unsqueeze(1).to_broadcast([P, 2, HEAD]),
-                            scalar=head_rinv[:, i, h : h + 1],
-                            in1=rope[norm][:, m],
-                            op0=ALU.mult,
-                            op1=ALU.mult,
-                        )
-                    nc.gpsimd.tensor_tensor(
-                        out=result[:, :, m, :].rearrange("p h (s j) -> p h s j", s=2),
-                        in0=terms[:, :, 0, :].rearrange("p h (s j) -> p h s j", s=2),
-                        in1=terms[:, :, 1, :].rearrange("p h (s j) -> p h s j", s=2)[:, :, ::-1, :],
-                        op=ALU.add,
-                    )
-                if m == TILES - 1:
-                    out, first_head = block[3], block[4]
-                    queue = nc.scalar if norm is None else nc.sync
-                    queue.dma_start(
-                        out=out.rearrange("b h (p m) d -> p (b h) (m d)", m=TILES)[
-                            :, first_head : first_head + HEADS, :
-                        ],
-                        in_=result[:].rearrange("p h m d -> p h (m d)"),
-                    )
+        def finish(step, next_rms):
+            block, m, product, rinv = step
+            terms = stage.tile([P, HEADS, 2, HEAD], F32, bufs=6, tag="terms")
+            rope_heads(block, m, product, rinv, terms, 0, HEADS // 2)
+            next_rinv = head_rinv(next_rms) if next_rms is not None else None
+            rope_heads(block, m, product, rinv, terms, HEADS // 2, HEADS)
+            rope_sum(block, m, terms)
+            if m == TILES - 1:
+                store(block, nc.sync)
+            return next_rinv
 
-        steps = []
-        for m in range(TILES):
-            steps.append((blocks[:PAIR], m))
+        steps = [(b0, 1), (b1, 1), (b0, 2), (b1, 2)]
         for block in blocks[PAIR:]:
             for m in range(TILES):
-                steps.append(([block], m))
-        held = None
-        for group, m in steps:
-            products, head_rinv = products_and_norms(group, m)
-            if held is not None:
-                rope_and_store(*held)
-            held = (group, m, products, head_rinv)
-        rope_and_store(*held)
+                steps.append((block, m))
+        for j, (block, m) in enumerate(steps):
+            if j == 0:
+                product = p01
+            else:
+                product = open_bank(block, m)
+                passes(block, m, product, 0, PASSES)
+            if block[5] is None:
+                if held is not None:
+                    finish(held, None)
+                    held = None
+                nc.scalar.copy(out=finished[block[2]][:, :, m, :], in_=product[:])
+                if m == TILES - 1:
+                    store(block, nc.scalar)
+            else:
+                rms = head_rms(product)
+                held = (block, m, product, finish(held, rms))

@@ -27,6 +27,7 @@ HEADS = N_BLOCK // HEAD
 N_ALL = 4096
 QUADRANT = 32
 LIVE = PASSES * 4
+S_SHARE = 1280
 PAIR = 2
 
 FLOPS = 2 * TOKENS * D_MODEL * N_ALL
@@ -77,21 +78,17 @@ def tile_rawkvinjector_pa_kernel(
         cos_rows = keep.tile([P, TILES, HEAD], BF16)
         sin_rows = keep.tile([P, TILES, HEAD], BF16)
 
-        nc.gpsimd.memset(weight_rows[:].bitcast(I32), 0)
         nc.vector.memset(eps[:], EPS)
-        nc.scalar.activation(out=table_warm[:], in_=eps[:], func=ACT.Sqrt)
+        nc.vector.memset(weight_rows[:].bitcast(I32), 0)
         nc.vector.memset(ones[:], 1.0)
         nc.vector.memset(w_planes[:].bitcast(I32), 0)
-        make_identity(nc, identity[:])
-
+        nc.scalar.activation(out=table_warm[:], in_=eps[:], func=ACT.Sqrt)
         nc.sync.dma_start(out=x_all[:, 0, :], in_=x_rows[:, 0, :])
-        nc.sync.dma_start(out=weight_rows[0:1, :D_MODEL], in_=ln1_w.unsqueeze(0))
         nc.sync.dma_start(out=x_all[:, 1, :], in_=x_rows[:, 1, :])
-        nc.sync.dma_start(out=x_all[:, 2, :], in_=x_rows[:, 2, :])
-        nc.sync.dma_start(out=weight_rows[0:1, D_MODEL : D_MODEL + HEAD], in_=q_norm_w.unsqueeze(0))
-        nc.sync.dma_start(out=weight_rows[0:1, D_MODEL + HEAD :], in_=k_norm_w.unsqueeze(0))
+        nc.sync.dma_start(out=weight_rows[0:1, :D_MODEL], in_=ln1_w.unsqueeze(0))
         nc.gpsimd.dma_start(out=cos_rows[:], in_=cos.rearrange("(p m) d -> p m d", m=TILES))
         nc.gpsimd.dma_start(out=sin_rows[:], in_=sin.rearrange("(p m) d -> p m d", m=TILES))
+        make_identity(nc, identity[:])
 
         blocks = []
         plane_col = 0
@@ -113,6 +110,12 @@ def tile_rawkvinjector_pa_kernel(
                         .rearrange("p n t -> p (n t)")[:, PACK * n0 : PACK * (n0 + PAIR * N_BLOCK)]
                         .bitcast(I32),
                     )
+                    if not blocks and g == 0:
+                        nc.sync.dma_start(out=x_all[:, 2, :], in_=x_rows[:, 2, :])
+                        nc.sync.dma_start(
+                            out=weight_rows[0:1, D_MODEL : D_MODEL + HEAD], in_=q_norm_w.unsqueeze(0)
+                        )
+                        nc.sync.dma_start(out=weight_rows[0:1, D_MODEL + HEAD :], in_=k_norm_w.unsqueeze(0))
                 for i in range(PAIR):
                     blocks.append((w_words, i * N_BLOCK, plane_col, out, (n0 + i * N_BLOCK) // HEAD, norm))
                     plane_col += N_BLOCK
@@ -129,8 +132,6 @@ def tile_rawkvinjector_pa_kernel(
                     stop=True,
                 )
             ln_bank.append(spread)
-        norm_bank = sums.tile([P, 2 * HEAD], F32, tag="product")
-        nc.tensor.matmul(out=norm_bank[:], lhsT=ones[:], rhs=weight_rows[:, D_MODEL:], start=True, stop=True)
         norm_w = keep.tile([P, 2, HEAD], F32)
 
         x_sumsq = keep.tile([P, TILES], F32)
@@ -146,13 +147,13 @@ def tile_rawkvinjector_pa_kernel(
             grouped.append(grouped_m)
 
         def token_rms(m):
-            s_cols = D_MODEL // 2 if m == 0 else D_MODEL
+            s_cols = S_SHARE if m == 0 else D_MODEL
             squares = stage.tile([P, D_MODEL], BF16)
             nc.scalar.activation(
                 out=squares[:, :s_cols], in_=x_all[:, m, :s_cols], func=ACT.Square, accum_out=x_sumsq[:, m : m + 1]
             )
             if m == 0:
-                v_squares = stage.tile([P, D_MODEL // 2], BF16)
+                v_squares = stage.tile([P, D_MODEL - S_SHARE], BF16)
                 nc.vector.scalar_tensor_tensor(
                     out=v_squares[:],
                     in0=x_all[:, m, s_cols:],
@@ -264,7 +265,7 @@ def tile_rawkvinjector_pa_kernel(
                     out=terms[:, h],
                     in0=product[:, h, :].unsqueeze(1).to_broadcast([P, 2, HEAD]),
                     scalar=rinv[:, h : h + 1],
-                    in1=rope[block[5]][:, m],
+                    in1=rope[:, m, block[5]],
                     op0=ALU.mult,
                     op1=ALU.mult,
                 )
@@ -284,6 +285,25 @@ def tile_rawkvinjector_pa_kernel(
                 in_=finished[block[2]][:].rearrange("p h m d -> p h (m d)"),
             )
 
+        minus_w = keep.tile([P, 2, HALF], F32)
+        rope = keep.tile([P, TILES, 2, 2, HEAD], F32)
+
+        def make_tables():
+            nc.gpsimd.tensor_scalar(
+                out=minus_w[:], in0=norm_w[:, :, HALF:], scalar1=-1.0, scalar2=0.0, op0=ALU.mult, op1=ALU.add
+            )
+            for out, in0, in1, width in (
+                (rope[:, :, :, 0, :], cos_rows[:], norm_w[:], HEAD),
+                (rope[:, :, :, 1, :HALF], sin_rows[:, :, HALF:], norm_w[:, :, :HALF], HALF),
+                (rope[:, :, :, 1, HALF:], sin_rows[:, :, :HALF], minus_w[:], HALF),
+            ):
+                nc.gpsimd.tensor_tensor(
+                    out=out,
+                    in0=in0.unsqueeze(2).to_broadcast([P, TILES, 2, width]),
+                    in1=in1.unsqueeze(1).to_broadcast([P, TILES, 2, width]),
+                    op=ALU.mult,
+                )
+
         b0, b1 = blocks[0], blocks[1]
         token_rms(0)
         token_rinv(0)
@@ -295,6 +315,11 @@ def tile_rawkvinjector_pa_kernel(
         group(0, 0, flipped00)
         token_rinv(1)
         quantise(0, 0, 2)
+        group(0, 1, flipped01)
+        norm_bank = sums.tile([P, 2 * HEAD], F32, tag="product")
+        nc.tensor.matmul(out=norm_bank[:], lhsT=ones[:], rhs=weight_rows[:, D_MODEL:], start=True, stop=True)
+        nc.scalar.copy(out=norm_w[:].rearrange("p n d -> p (n d)"), in_=norm_bank[:])
+        make_tables()
         token_rms(2)
         p00 = open_bank(b0, 0)
         p10 = open_bank(b1, 0)
@@ -304,14 +329,12 @@ def tile_rawkvinjector_pa_kernel(
         passes(b1, 0, p10, 1, 2)
         sorted10 = normalise(1, 0)
         flipped10 = flip(sorted10)
-        group(0, 1, flipped01)
+        quantise(0, 2, 4)
         sorted11 = normalise(1, 1)
         flipped11 = flip(sorted11)
-        quantise(0, 2, 4)
         token_rinv(2)
         passes(b0, 0, p00, 2, 4)
         passes(b1, 0, p10, 2, 4)
-        nc.scalar.copy(out=norm_w[:].rearrange("p n d -> p (n d)"), in_=norm_bank[:])
         group(1, 0, flipped10)
         group(1, 1, flipped11)
         sorted20 = normalise(2, 0)
@@ -325,31 +348,6 @@ def tile_rawkvinjector_pa_kernel(
         group(2, 0, flipped20)
         rms10 = head_rms(p10)
         group(2, 1, flipped21)
-
-        minus_w = keep.tile([P, 2, HALF], F32)
-        nc.gpsimd.tensor_scalar(
-            out=minus_w[:], in0=norm_w[:, :, HALF:], scalar1=-1.0, scalar2=0.0, op0=ALU.mult, op1=ALU.add
-        )
-        rope = []
-        for norm in range(2):
-            table = keep.tile([P, TILES, 2, HEAD], F32, name="rope%d" % norm)
-            w_all = norm_w[:, norm, :].unsqueeze(1)
-            nc.gpsimd.tensor_tensor(
-                out=table[:, :, 0, :], in0=cos_rows[:], in1=w_all.to_broadcast([P, TILES, HEAD]), op=ALU.mult
-            )
-            nc.gpsimd.tensor_tensor(
-                out=table[:, :, 1, :HALF],
-                in0=sin_rows[:, :, HALF:],
-                in1=w_all[:, :, :HALF].to_broadcast([P, TILES, HALF]),
-                op=ALU.mult,
-            )
-            nc.gpsimd.tensor_tensor(
-                out=table[:, :, 1, HALF:],
-                in0=sin_rows[:, :, :HALF],
-                in1=minus_w[:, norm, :].unsqueeze(1).to_broadcast([P, TILES, HALF]),
-                op=ALU.mult,
-            )
-            rope.append(table)
 
         rinv00 = head_rinv(rms00)
         terms00 = stage.tile([P, HEADS, 2, HEAD], F32, bufs=6, tag="terms")

@@ -69,23 +69,28 @@ def tile_rawkvinjector_pa_kernel(
 
         x_all = keep.tile([P, TILES, D_MODEL], BF16)
         x_rows = hidden_states.rearrange("b (p m) k -> p (b m) k", m=TILES)
-        weight_rows = keep.tile([P, D_MODEL + 2 * HEAD], BF16)
+        ln_rows = keep.tile([P, K_PASS], BF16)
+        norm_w = keep.tile([P, 2, HEAD], BF16)
         w_planes = keep.tile([P, N_ALL], U8, align_bytes=64)
         eps = keep.tile([P, 1], F32)
-        ones = keep.tile([P, P], BF16)
+        pick = keep.tile([P, PASSES], BF16)
         table_warm = keep.tile([P, 1], F32)
         identity = keep.tile([P, P], F32)
         cos_rows = keep.tile([P, TILES, HEAD], BF16)
         sin_rows = keep.tile([P, TILES, HEAD], BF16)
 
         nc.vector.memset(eps[:], EPS)
-        nc.vector.memset(weight_rows[:].bitcast(I32), 0)
-        nc.vector.memset(ones[:], 1.0)
+        nc.vector.memset(ln_rows[:].bitcast(I32), 0)
+        nc.vector.memset(pick[:], 0.0)
+        for g in range(PASSES):
+            nc.vector.memset(pick[g * QUADRANT : g * QUADRANT + 1, g : g + 1], 1.0)
         nc.vector.memset(w_planes[:].bitcast(I32), 0)
         nc.scalar.activation(out=table_warm[:], in_=eps[:], func=ACT.Sqrt)
         nc.sync.dma_start(out=x_all[:, 0, :], in_=x_rows[:, 0, :])
+        nc.sync.dma_start(out=ln_rows[0:P:QUADRANT, :], in_=ln1_w.rearrange("(g n) -> g n", g=PASSES))
+        nc.sync.dma_start(out=norm_w[:, 0, :], in_=q_norm_w.partition_broadcast(P))
+        nc.sync.dma_start(out=norm_w[:, 1, :], in_=k_norm_w.partition_broadcast(P))
         nc.sync.dma_start(out=x_all[:, 1, :], in_=x_rows[:, 1, :])
-        nc.sync.dma_start(out=weight_rows[0:1, :D_MODEL], in_=ln1_w.unsqueeze(0))
         nc.gpsimd.dma_start(out=cos_rows[:], in_=cos.rearrange("(p m) d -> p m d", m=TILES))
         nc.gpsimd.dma_start(out=sin_rows[:], in_=sin.rearrange("(p m) d -> p m d", m=TILES))
         make_identity(nc, identity[:])
@@ -102,22 +107,34 @@ def tile_rawkvinjector_pa_kernel(
                     in_=scales[:, 4 * quad : 4 * quad + 4, :].bitcast(I32),
                 )
             for n0 in range(0, words.shape[2], PAIR * N_BLOCK):
-                w_words = keep.tile([P, PASSES, PAIR * N_BLOCK], U32, name="w_words%d" % plane_col, align_bytes=64)
-                for g in range(PASSES):
-                    nc.sync.dma_start(
-                        out=w_words[:, g, :].bitcast(I32),
-                        in_=words[g]
-                        .rearrange("p n t -> p (n t)")[:, PACK * n0 : PACK * (n0 + PAIR * N_BLOCK)]
-                        .bitcast(I32),
-                    )
-                    if not blocks and g == 0:
-                        nc.sync.dma_start(out=x_all[:, 2, :], in_=x_rows[:, 2, :])
+                w_tiles = []
+                if norm == 0:
+                    for i in range(PAIR):
+                        w_block = keep.tile([P, PASSES, N_BLOCK], U32, name="q_words%d" % (plane_col + i), align_bytes=64)
+                        w_tiles.append((w_block, 0))
+                        for g in range(0, PASSES, 2):
+                            nc.sync.dma_start(
+                                out=w_block[:, g : g + 2, :].bitcast(I32),
+                                in_=words[g : g + 2]
+                                .rearrange("g p n t -> p g (n t)")[
+                                    :, :, PACK * (n0 + i * N_BLOCK) : PACK * (n0 + (i + 1) * N_BLOCK)
+                                ]
+                                .bitcast(I32),
+                            )
+                            if not blocks and i == 0 and g == 0:
+                                nc.sync.dma_start(out=x_all[:, 2, :], in_=x_rows[:, 2, :])
+                else:
+                    w_words = keep.tile([P, PASSES, PAIR * N_BLOCK], U32, name="w_words%d" % plane_col, align_bytes=64)
+                    w_tiles += [(w_words, 0), (w_words, N_BLOCK)]
+                    for g in range(PASSES):
                         nc.sync.dma_start(
-                            out=weight_rows[0:1, D_MODEL : D_MODEL + HEAD], in_=q_norm_w.unsqueeze(0)
+                            out=w_words[:, g, :].bitcast(I32),
+                            in_=words[g]
+                            .rearrange("p n t -> p (n t)")[:, PACK * n0 : PACK * (n0 + PAIR * N_BLOCK)]
+                            .bitcast(I32),
                         )
-                        nc.sync.dma_start(out=weight_rows[0:1, D_MODEL + HEAD :], in_=k_norm_w.unsqueeze(0))
                 for i in range(PAIR):
-                    blocks.append((w_words, i * N_BLOCK, plane_col, out, (n0 + i * N_BLOCK) // HEAD, norm))
+                    blocks.append((w_tiles[i][0], w_tiles[i][1], plane_col, out, (n0 + i * N_BLOCK) // HEAD, norm))
                     plane_col += N_BLOCK
 
         ln_bank = []
@@ -126,13 +143,12 @@ def tile_rawkvinjector_pa_kernel(
             for i in range(2):
                 nc.tensor.matmul(
                     out=spread[:, i * K_PASS : (i + 1) * K_PASS],
-                    lhsT=ones[:],
-                    rhs=weight_rows[:, (first + i) * K_PASS : (first + i + 1) * K_PASS],
+                    lhsT=pick[:, first + i : first + i + 1].to_broadcast([P, P]),
+                    rhs=ln_rows[:],
                     start=True,
                     stop=True,
                 )
             ln_bank.append(spread)
-        norm_w = keep.tile([P, 2, HEAD], F32)
 
         x_sumsq = keep.tile([P, TILES], F32)
         x_rms = keep.tile([P, TILES], F32)
@@ -177,12 +193,13 @@ def tile_rawkvinjector_pa_kernel(
         def token_rinv(m):
             nc.vector.reciprocal(out=x_rinv[:, m : m + 1], in_=x_rms[:, m : m + 1])
 
-        def normalise(m, half):
-            h_sorted = stage.tile([P, 2, 2 * P, 2], BF16, bufs=4)
+        def normalise(m, half, parts=(0, 1), h_sorted=None):
+            if h_sorted is None:
+                h_sorted = stage.tile([P, 2, 2 * P, 2], BF16, bufs=4)
             k_range = slice(half * 2 * K_PASS, (half + 1) * 2 * K_PASS)
             x_pairs = x_all[:, m, k_range].rearrange("r (q u e) -> r u q e", u=2, e=2)
             ln_pairs = ln_bank[half][:].rearrange("r (q u e) -> r u q e", u=2, e=2)
-            for u in range(2):
+            for u in parts:
                 nc.vector.scalar_tensor_tensor(
                     out=h_sorted[:, u],
                     in0=x_pairs[:, u],
@@ -292,71 +309,15 @@ def tile_rawkvinjector_pa_kernel(
             nc.gpsimd.tensor_scalar(
                 out=minus_w[:], in0=norm_w[:, :, HALF:], scalar1=-1.0, scalar2=0.0, op0=ALU.mult, op1=ALU.add
             )
-            for out, in0, in1, width in (
-                (rope[:, :, :, 0, :], cos_rows[:], norm_w[:], HEAD),
-                (rope[:, :, :, 1, :HALF], sin_rows[:, :, HALF:], norm_w[:, :, :HALF], HALF),
-                (rope[:, :, :, 1, HALF:], sin_rows[:, :, :HALF], minus_w[:], HALF),
-            ):
-                nc.gpsimd.tensor_tensor(
-                    out=out,
-                    in0=in0.unsqueeze(2).to_broadcast([P, TILES, 2, width]),
-                    in1=in1.unsqueeze(1).to_broadcast([P, TILES, 2, width]),
-                    op=ALU.mult,
-                )
-
-        b0, b1 = blocks[0], blocks[1]
-        token_rms(0)
-        token_rinv(0)
-        token_rms(1)
-        sorted00 = normalise(0, 0)
-        flipped00 = flip(sorted00)
-        sorted01 = normalise(0, 1)
-        flipped01 = flip(sorted01)
-        group(0, 0, flipped00)
-        token_rinv(1)
-        quantise(0, 0, 2)
-        group(0, 1, flipped01)
-        norm_bank = sums.tile([P, 2 * HEAD], F32, tag="product")
-        nc.tensor.matmul(out=norm_bank[:], lhsT=ones[:], rhs=weight_rows[:, D_MODEL:], start=True, stop=True)
-        nc.scalar.copy(out=norm_w[:].rearrange("p n d -> p (n d)"), in_=norm_bank[:])
-        make_tables()
-        token_rms(2)
-        p00 = open_bank(b0, 0)
-        p10 = open_bank(b1, 0)
-        passes(b0, 0, p00, 0, 1)
-        passes(b1, 0, p10, 0, 1)
-        passes(b0, 0, p00, 1, 2)
-        passes(b1, 0, p10, 1, 2)
-        sorted10 = normalise(1, 0)
-        flipped10 = flip(sorted10)
-        quantise(0, 2, 4)
-        sorted11 = normalise(1, 1)
-        flipped11 = flip(sorted11)
-        token_rinv(2)
-        passes(b0, 0, p00, 2, 4)
-        passes(b1, 0, p10, 2, 4)
-        group(1, 0, flipped10)
-        group(1, 1, flipped11)
-        sorted20 = normalise(2, 0)
-        flipped20 = flip(sorted20)
-        quantise(1, 0, 4)
-        rms00 = head_rms(p00)
-        p01 = open_bank(b0, 1)
-        passes(b0, 1, p01, 0, 4)
-        sorted21 = normalise(2, 1)
-        flipped21 = flip(sorted21)
-        group(2, 0, flipped20)
-        rms10 = head_rms(p10)
-        group(2, 1, flipped21)
-
-        rinv00 = head_rinv(rms00)
-        terms00 = stage.tile([P, HEADS, 2, HEAD], F32, bufs=6, tag="terms")
-        rope_heads(b0, 0, p00, rinv00, terms00, 0, HEADS)
-        rope_sum(b0, 0, terms00)
-        rinv10 = head_rinv(rms10)
-        quantise(2, 0, 4)
-
-        held = (b1, 0, p10, rinv10)
+            for norm in range(2):
+                for out, in0, in1, width in (
+                    (rope[:, :, norm, 0, :], cos_rows[:], norm_w[:, norm, :], HEAD),
+                    (rope[:, :, norm, 1, :HALF], sin_rows[:, :, HALF:], norm_w[:, norm, :HALF], HALF),
+                    (rope[:, :, norm, 1, HALF:], sin_rows[:, :, :HALF], minus_w[:, norm, :], HALF),
+                ):
+                    nc.gpsimd.tensor_tensor(
+                        out=out, in0=in0, in1=in1.unsqueeze(1).to_broadcast([P, TILES, width]), op=ALU.mult
+                    )
 
         def finish(step, next_rms):
             block, m, product, rinv = step
@@ -369,13 +330,61 @@ def tile_rawkvinjector_pa_kernel(
                 store(block, nc.sync)
             return next_rinv
 
-        steps = [(b0, 1), (b1, 1), (b0, 2), (b1, 2)]
-        for block in blocks[PAIR:]:
+        b0, b1 = blocks[0], blocks[1]
+        make_tables()
+        token_rms(0)
+        token_rinv(0)
+        token_rms(1)
+        sorted00 = normalise(0, 0)
+        flipped00 = flip(sorted00)
+        sorted01 = normalise(0, 1)
+        flipped01 = flip(sorted01)
+        group(0, 0, flipped00)
+        token_rinv(1)
+        sorted10 = normalise(1, 0, (0,))
+        quantise(0, 0, 2)
+        group(0, 1, flipped01)
+        token_rms(2)
+        p00 = open_bank(b0, 0)
+        passes(b0, 0, p00, 0, 2)
+        normalise(1, 0, (1,), sorted10)
+        flipped10 = flip(sorted10)
+        sorted11 = normalise(1, 1)
+        flipped11 = flip(sorted11)
+        quantise(0, 2, 4)
+        token_rinv(2)
+        passes(b0, 0, p00, 2, 4)
+        p10 = open_bank(b1, 0)
+        passes(b1, 0, p10, 0, 4)
+        group(1, 0, flipped10)
+        group(1, 1, flipped11)
+        sorted20 = normalise(2, 0)
+        flipped20 = flip(sorted20)
+        quantise(1, 0, 4)
+        rms00 = head_rms(p00)
+        p01 = open_bank(b0, 1)
+        passes(b0, 1, p01, 0, 4)
+        group(2, 0, flipped20)
+        sorted21 = normalise(2, 1)
+        flipped21 = flip(sorted21)
+        rms10 = head_rms(p10)
+        group(2, 1, flipped21)
+        p11 = open_bank(b1, 1)
+        passes(b1, 1, p11, 0, 4)
+        rinv10 = finish((b0, 0, p00, head_rinv(rms00)), rms10)
+        rms01 = head_rms(p01)
+        rinv01 = finish((b1, 0, p10, rinv10), rms01)
+        quantise(2, 0, 4)
+        held = (b0, 1, p01, rinv01)
+
+        b2 = blocks[PAIR]
+        steps = [(b1, 1), (b2, 0), (b0, 2), (b1, 2), (b2, 1), (b2, 2)]
+        for block in blocks[PAIR + 1 :]:
             for m in range(TILES):
                 steps.append((block, m))
         for j, (block, m) in enumerate(steps):
-            if j == 0:
-                product = p01
+            if j < 1:
+                product = (p11,)[j]
             else:
                 product = open_bank(block, m)
                 passes(block, m, product, 0, PASSES)
@@ -388,4 +397,4 @@ def tile_rawkvinjector_pa_kernel(
                     store(block, nc.scalar)
             else:
                 rms = head_rms(product)
-                held = (block, m, product, finish(held, rms))
+                held = (block, m, product, finish(held, rms) if held is not None else head_rinv(rms))

@@ -70,7 +70,8 @@ def tile_rawkvinjector_pa_kernel(
         x_all = keep.tile([P, TILES, D_MODEL], BF16)
         x_rows = hidden_states.rearrange("b (p m) k -> p (b m) k", m=TILES)
         ln_rows = keep.tile([P, K_PASS], BF16)
-        norm_w = keep.tile([P, 2, HEAD], BF16)
+        norm_rows = keep.tile([P, 2 * HEAD], BF16)
+        norm_w = keep.tile([P, 2, HEAD], F32)
         w_planes = keep.tile([P, N_ALL], U8, align_bytes=64)
         eps = keep.tile([P, 1], F32)
         pick = keep.tile([P, PASSES], BF16)
@@ -81,16 +82,15 @@ def tile_rawkvinjector_pa_kernel(
 
         nc.vector.memset(eps[:], EPS)
         nc.vector.memset(ln_rows[:].bitcast(I32), 0)
+        nc.vector.memset(norm_rows[:].bitcast(I32), 0)
         nc.vector.memset(pick[:], 0.0)
         for g in range(PASSES):
             nc.vector.memset(pick[g * QUADRANT : g * QUADRANT + 1, g : g + 1], 1.0)
         nc.vector.memset(w_planes[:].bitcast(I32), 0)
         nc.scalar.activation(out=table_warm[:], in_=eps[:], func=ACT.Sqrt)
         nc.sync.dma_start(out=x_all[:, 0, :], in_=x_rows[:, 0, :])
-        nc.sync.dma_start(out=ln_rows[0:P:QUADRANT, :], in_=ln1_w.rearrange("(g n) -> g n", g=PASSES))
-        nc.sync.dma_start(out=norm_w[:, 0, :], in_=q_norm_w.partition_broadcast(P))
-        nc.sync.dma_start(out=norm_w[:, 1, :], in_=k_norm_w.partition_broadcast(P))
         nc.sync.dma_start(out=x_all[:, 1, :], in_=x_rows[:, 1, :])
+        nc.sync.dma_start(out=ln_rows[0:P:QUADRANT, :], in_=ln1_w.rearrange("(g n) -> g n", g=PASSES))
         nc.gpsimd.dma_start(out=cos_rows[:], in_=cos.rearrange("(p m) d -> p m d", m=TILES))
         nc.gpsimd.dma_start(out=sin_rows[:], in_=sin.rearrange("(p m) d -> p m d", m=TILES))
         make_identity(nc, identity[:])
@@ -123,6 +123,8 @@ def tile_rawkvinjector_pa_kernel(
                             )
                             if not blocks and i == 0 and g == 0:
                                 nc.sync.dma_start(out=x_all[:, 2, :], in_=x_rows[:, 2, :])
+                                nc.sync.dma_start(out=norm_rows[0:1, :HEAD], in_=q_norm_w.unsqueeze(0))
+                                nc.sync.dma_start(out=norm_rows[0:1, HEAD:], in_=k_norm_w.unsqueeze(0))
                 else:
                     w_words = keep.tile([P, PASSES, PAIR * N_BLOCK], U32, name="w_words%d" % plane_col, align_bytes=64)
                     w_tiles += [(w_words, 0), (w_words, N_BLOCK)]
@@ -230,6 +232,13 @@ def tile_rawkvinjector_pa_kernel(
                 in_=grouped[m][:, g0:g1].rearrange("p g r u -> p (g r u)").bitcast(BF16),
             )
 
+        def spread_norms():
+            norm_bank = sums.tile([P, 2 * HEAD], F32, tag="product")
+            nc.tensor.matmul(
+                out=norm_bank[:], lhsT=pick[:, 0:1].to_broadcast([P, P]), rhs=norm_rows[:], start=True, stop=True
+            )
+            nc.scalar.copy(out=norm_w[:].rearrange("p n d -> p (n d)"), in_=norm_bank[:])
+
         finished = {}
         opened = []
 
@@ -331,7 +340,6 @@ def tile_rawkvinjector_pa_kernel(
             return next_rinv
 
         b0, b1 = blocks[0], blocks[1]
-        make_tables()
         token_rms(0)
         token_rinv(0)
         token_rms(1)
@@ -345,6 +353,8 @@ def tile_rawkvinjector_pa_kernel(
         quantise(0, 0, 2)
         group(0, 1, flipped01)
         token_rms(2)
+        spread_norms()
+        make_tables()
         p00 = open_bank(b0, 0)
         passes(b0, 0, p00, 0, 2)
         normalise(1, 0, (1,), sorted10)

@@ -89,8 +89,8 @@ def tile_rawkvinjector_pa_kernel(
         nc.vector.memset(w_planes[:].bitcast(I32), 0)
         nc.scalar.activation(out=table_warm[:], in_=eps[:], func=ACT.Sqrt)
         nc.sync.dma_start(out=x_all[:, 0, :], in_=x_rows[:, 0, :])
-        nc.sync.dma_start(out=x_all[:, 1, :], in_=x_rows[:, 1, :])
         nc.sync.dma_start(out=ln_rows[0:P:QUADRANT, :], in_=ln1_w.rearrange("(g n) -> g n", g=PASSES))
+        nc.sync.dma_start(out=x_all[:, 1, :], in_=x_rows[:, 1, :])
         nc.gpsimd.dma_start(out=cos_rows[:], in_=cos.rearrange("(p m) d -> p m d", m=TILES))
         nc.gpsimd.dma_start(out=sin_rows[:], in_=sin.rearrange("(p m) d -> p m d", m=TILES))
         make_identity(nc, identity[:])
@@ -248,20 +248,21 @@ def tile_rawkvinjector_pa_kernel(
             else:
                 product = sums.tile([P, HEADS, HEAD], F32)
             opened.append(product)
-            if m == 0:
+            if block[2] not in finished:
                 result = results.tile([P, HEADS, TILES, HEAD], F32)
                 finished[block[2]] = result
             return product
 
-        def passes(block, m, product, g0, g1):
-            w_words, words_col, plane_col = block[0], block[1], block[2]
+        def passes(block, m, product, g0, g1, h0=0, h1=HEADS):
+            w_words, words_col, plane_col = block[0], block[1] + h0 * HEAD, block[2] + h0 * HEAD
+            n = (h1 - h0) * HEAD
             for g in range(g0, g1):
                 nc.tensor.matmul_mx(
-                    out=product[:].rearrange("p h d -> p (h d)"),
+                    out=product[:, : h1 - h0, :].rearrange("p h d -> p (h d)"),
                     lhsT=h_words[:, m, g, :].bitcast(FP8X4),
                     lhsT_scale=h_planes[:, m, g, :],
-                    rhs=w_words[:, g, words_col : words_col + N_BLOCK].bitcast(FP8X4),
-                    rhs_scale=w_planes[4 * g : P, plane_col : plane_col + N_BLOCK],
+                    rhs=w_words[:, g, words_col : words_col + n].bitcast(FP8X4),
+                    rhs_scale=w_planes[4 * g : P, plane_col : plane_col + n],
                     start=(g == 0),
                     stop=(g == PASSES - 1),
                 )
@@ -296,19 +297,19 @@ def tile_rawkvinjector_pa_kernel(
                     op1=ALU.mult,
                 )
 
-        def rope_sum(block, m, terms):
+        def rope_sum(block, m, terms, h0=0, h1=HEADS):
             nc.gpsimd.tensor_tensor(
-                out=finished[block[2]][:, :, m, :].rearrange("p h (s j) -> p h s j", s=2),
-                in0=terms[:, :, 0, :].rearrange("p h (s j) -> p h s j", s=2),
-                in1=terms[:, :, 1, :].rearrange("p h (s j) -> p h s j", s=2)[:, :, ::-1, :],
+                out=finished[block[2]][:, h0:h1, m, :].rearrange("p h (s j) -> p h s j", s=2),
+                in0=terms[:, h0:h1, 0, :].rearrange("p h (s j) -> p h s j", s=2),
+                in1=terms[:, h0:h1, 1, :].rearrange("p h (s j) -> p h s j", s=2)[:, :, ::-1, :],
                 op=ALU.add,
             )
 
-        def store(block, queue):
+        def store(block, queue, h0=0, h1=HEADS):
             out, first_head = block[3], block[4]
             queue.dma_start(
-                out=out.rearrange("b h (p m) d -> p (b h) (m d)", m=TILES)[:, first_head : first_head + HEADS, :],
-                in_=finished[block[2]][:].rearrange("p h m d -> p h (m d)"),
+                out=out.rearrange("b h (p m) d -> p (b h) (m d)", m=TILES)[:, first_head + h0 : first_head + h1, :],
+                in_=finished[block[2]][:, h0:h1].rearrange("p h m d -> p h (m d)"),
             )
 
         minus_w = keep.tile([P, 2, HALF], F32)
@@ -332,7 +333,14 @@ def tile_rawkvinjector_pa_kernel(
             block, m, product, rinv = step
             terms = stage.tile([P, HEADS, 2, HEAD], F32, bufs=6, tag="terms")
             rope_heads(block, m, product, rinv, terms, 0, HEADS // 2)
-            next_rinv = head_rinv(next_rms) if next_rms is not None else None
+            if next_rms is None:
+                rope_sum(block, m, terms, 0, HEADS // 2)
+                store(block, nc.sync, 0, HEADS // 2)
+                rope_heads(block, m, product, rinv, terms, HEADS // 2, HEADS)
+                rope_sum(block, m, terms, HEADS // 2, HEADS)
+                store(block, nc.sync, HEADS // 2, HEADS)
+                return None
+            next_rinv = head_rinv(next_rms)
             rope_heads(block, m, product, rinv, terms, HEADS // 2, HEADS)
             rope_sum(block, m, terms)
             if m == TILES - 1:
@@ -388,23 +396,29 @@ def tile_rawkvinjector_pa_kernel(
         held = (b0, 1, p01, rinv01)
 
         b2 = blocks[PAIR]
-        steps = [(b1, 1), (b2, 0), (b0, 2), (b1, 2), (b2, 1), (b2, 2)]
-        for block in blocks[PAIR + 1 :]:
+        b3, k0, k1, v0, v1 = blocks[PAIR + 1 :]
+        steps = [(b1, 1), (b2, 0), (b2, 1), (b0, 2), (b1, 2), (b2, 2)]
+        for block in (b3, k0, v0, k1):
             for m in range(TILES):
                 steps.append((block, m))
         for j, (block, m) in enumerate(steps):
-            if j < 1:
-                product = (p11,)[j]
+            if j == 0:
+                product = p11
             else:
                 product = open_bank(block, m)
                 passes(block, m, product, 0, PASSES)
             if block[5] is None:
-                if held is not None:
-                    finish(held, None)
-                    held = None
                 nc.scalar.copy(out=finished[block[2]][:, :, m, :], in_=product[:])
                 if m == TILES - 1:
                     store(block, nc.scalar)
             else:
                 rms = head_rms(product)
-                held = (block, m, product, finish(held, rms) if held is not None else head_rinv(rms))
+                held = (block, m, product, finish(held, rms))
+        finish(held, None)
+        for h0 in range(0, HEADS, HEADS // 2):
+            h1 = h0 + HEADS // 2
+            for m in range(TILES):
+                product = open_bank(v1, m)
+                passes(v1, m, product, 0, PASSES, h0, h1)
+                nc.scalar.copy(out=finished[v1[2]][:, h0:h1, m, :], in_=product[:, : h1 - h0, :])
+            store(v1, nc.scalar, h0, h1)

@@ -88,7 +88,8 @@ def tile_rawkvinjector_pa_kernel(
             nc.vector.memset(pick[g * QUADRANT : g * QUADRANT + 1, g : g + 1], 1.0)
         nc.vector.memset(w_planes[:].bitcast(I32), 0)
         nc.scalar.activation(out=table_warm[:], in_=eps[:], func=ACT.Sqrt)
-        nc.sync.dma_start(out=x_all[:, 0, :], in_=x_rows[:, 0, :])
+        nc.sync.dma_start(out=x_all[:, 0, :S_SHARE], in_=x_rows[:, 0, :S_SHARE])
+        nc.sync.dma_start(out=x_all[:, 0, S_SHARE:], in_=x_rows[:, 0, S_SHARE:])
         nc.sync.dma_start(out=ln_rows[0:P:QUADRANT, :], in_=ln1_w.rearrange("(g n) -> g n", g=PASSES))
         nc.sync.dma_start(out=x_all[:, 1, :], in_=x_rows[:, 1, :])
         nc.gpsimd.dma_start(out=cos_rows[:], in_=cos.rearrange("(p m) d -> p m d", m=TILES))
@@ -394,6 +395,7 @@ def tile_rawkvinjector_pa_kernel(
         rinv01 = finish((b1, 0, p10, rinv10), rms01)
         quantise(2, 0, 4)
         held = (b0, 1, p01, rinv01)
+
 
         b2 = blocks[PAIR]
         b3, k0, k1, v0, v1 = blocks[PAIR + 1 :]

@@ -96,49 +96,46 @@ def tile_rawkvinjector_pa_kernel(
         nc.gpsimd.dma_start(out=sin_rows[:], in_=sin.rearrange("(p m) d -> p m d", m=TILES))
         make_identity(nc, identity[:])
 
-        blocks = []
-        plane_col = 0
-        for words, scales, out, norm in projections:
-            n_cols = scales.shape[2]
+        plane_cols = (0, Wq_words.shape[2], Wq_words.shape[2] + Wk_words.shape[2])
+
+        def load_scales(which):
+            scales, n_cols = projections[which][1], projections[which][1].shape[2]
             for quad in range(P // QUADRANT):
                 nc.sync.dma_start(
                     out=w_planes[
-                        quad * QUADRANT : quad * QUADRANT + LIVE, plane_col : plane_col + n_cols
+                        quad * QUADRANT : quad * QUADRANT + LIVE, plane_cols[which] : plane_cols[which] + n_cols
                     ].bitcast(I32),
                     in_=scales[:, 4 * quad : 4 * quad + 4, :].bitcast(I32),
                 )
-            for n0 in range(0, words.shape[2], PAIR * N_BLOCK):
-                w_tiles = []
-                if norm == 0:
-                    for i in range(PAIR):
-                        w_block = keep.tile([P, PASSES, N_BLOCK], U32, name="q_words%d" % (plane_col + i), align_bytes=64)
-                        w_tiles.append((w_block, 0))
-                        for g in range(0, PASSES, 2):
-                            nc.sync.dma_start(
-                                out=w_block[:, g : g + 2, :].bitcast(I32),
-                                in_=words[g : g + 2]
-                                .rearrange("g p n t -> p g (n t)")[
-                                    :, :, PACK * (n0 + i * N_BLOCK) : PACK * (n0 + (i + 1) * N_BLOCK)
-                                ]
-                                .bitcast(I32),
-                            )
-                            if not blocks and i == 0 and g == 0:
-                                nc.sync.dma_start(out=x_all[:, 2, :], in_=x_rows[:, 2, :])
-                                nc.sync.dma_start(out=norm_rows[0:1, :HEAD], in_=q_norm_w.unsqueeze(0))
-                                nc.sync.dma_start(out=norm_rows[0:1, HEAD:], in_=k_norm_w.unsqueeze(0))
-                else:
-                    w_words = keep.tile([P, PASSES, PAIR * N_BLOCK], U32, name="w_words%d" % plane_col, align_bytes=64)
-                    w_tiles += [(w_words, 0), (w_words, N_BLOCK)]
-                    for g in range(PASSES):
-                        nc.sync.dma_start(
-                            out=w_words[:, g, :].bitcast(I32),
-                            in_=words[g]
-                            .rearrange("p n t -> p (n t)")[:, PACK * n0 : PACK * (n0 + PAIR * N_BLOCK)]
-                            .bitcast(I32),
-                        )
-                for i in range(PAIR):
-                    blocks.append((w_tiles[i][0], w_tiles[i][1], plane_col, out, (n0 + i * N_BLOCK) // HEAD, norm))
-                    plane_col += N_BLOCK
+
+        def load_words(which, first, count, passes_each):
+            words, scales, out, norm = projections[which]
+            tile = keep.tile([P, PASSES, count * N_BLOCK], U32, name="words%d_%d" % (which, first), align_bytes=64)
+            for g in range(0, PASSES, passes_each):
+                nc.sync.dma_start(
+                    out=tile[:, g : g + passes_each, :].bitcast(I32),
+                    in_=words[g : g + passes_each]
+                    .rearrange("g p n t -> p g (n t)")[
+                        :, :, PACK * first * N_BLOCK : PACK * (first + count) * N_BLOCK
+                    ]
+                    .bitcast(I32),
+                )
+            return [
+                (tile, i * N_BLOCK, plane_cols[which] + (first + i) * N_BLOCK, out, (first + i) * HEADS, norm)
+                for i in range(count)
+            ]
+
+        load_scales(0)
+        nc.sync.dma_start(out=x_all[:, 2, :], in_=x_rows[:, 2, :])
+        nc.sync.dma_start(out=norm_rows[0:1, :HEAD], in_=q_norm_w.unsqueeze(0))
+        nc.sync.dma_start(out=norm_rows[0:1, HEAD:], in_=k_norm_w.unsqueeze(0))
+        b0, b1 = load_words(0, 0, 2, 1)
+        (b2,) = load_words(0, 2, 1, 2)
+        (b3,) = load_words(0, 3, 1, 4)
+        load_scales(1)
+        k0, k1 = load_words(1, 0, 2, 2)
+        load_scales(2)
+        v0, v1 = load_words(2, 0, 2, 2)
 
         ln_bank = []
         for first in range(0, PASSES, 2):
@@ -348,7 +345,6 @@ def tile_rawkvinjector_pa_kernel(
                 store(block, nc.sync)
             return next_rinv
 
-        b0, b1 = blocks[0], blocks[1]
         token_rms(0)
         token_rinv(0)
         token_rms(1)
@@ -365,16 +361,18 @@ def tile_rawkvinjector_pa_kernel(
         spread_norms()
         make_tables()
         p00 = open_bank(b0, 0)
-        passes(b0, 0, p00, 0, 2)
+        p10 = open_bank(b1, 0)
+        passes(b0, 0, p00, 0, 1)
+        passes(b1, 0, p10, 0, 1)
         normalise(1, 0, (1,), sorted10)
         flipped10 = flip(sorted10)
         sorted11 = normalise(1, 1)
         flipped11 = flip(sorted11)
         quantise(0, 2, 4)
         token_rinv(2)
-        passes(b0, 0, p00, 2, 4)
-        p10 = open_bank(b1, 0)
-        passes(b1, 0, p10, 0, 4)
+        for g in range(1, PASSES):
+            passes(b0, 0, p00, g, g + 1)
+            passes(b1, 0, p10, g, g + 1)
         group(1, 0, flipped10)
         group(1, 1, flipped11)
         sorted20 = normalise(2, 0)
@@ -395,20 +393,16 @@ def tile_rawkvinjector_pa_kernel(
         rinv01 = finish((b1, 0, p10, rinv10), rms01)
         quantise(2, 0, 4)
         held = (b0, 1, p01, rinv01)
+        rms11 = head_rms(p11)
+        held = (b1, 1, p11, finish(held, rms11))
 
-
-        b2 = blocks[PAIR]
-        b3, k0, k1, v0, v1 = blocks[PAIR + 1 :]
-        steps = [(b1, 1), (b2, 0), (b2, 1), (b0, 2), (b1, 2), (b2, 2)]
+        steps = [(b2, 0), (b2, 1), (b0, 2), (b1, 2), (b2, 2)]
         for block in (b3, k0, v0, k1):
             for m in range(TILES):
                 steps.append((block, m))
-        for j, (block, m) in enumerate(steps):
-            if j == 0:
-                product = p11
-            else:
-                product = open_bank(block, m)
-                passes(block, m, product, 0, PASSES)
+        for block, m in steps:
+            product = open_bank(block, m)
+            passes(block, m, product, 0, PASSES)
             if block[5] is None:
                 nc.scalar.copy(out=finished[block[2]][:, :, m, :], in_=product[:])
                 if m == TILES - 1:

@@ -120,6 +120,9 @@ def tile_rawkvinjector_pa_kernel(
                     ]
                     .bitcast(I32),
                 )
+                if which == 0 and first == 0 and g == 0:
+                    nc.sync.dma_start(out=norm_rows[0:1, :HEAD], in_=q_norm_w.unsqueeze(0))
+                    nc.sync.dma_start(out=norm_rows[0:1, HEAD:], in_=k_norm_w.unsqueeze(0))
             return [
                 (tile, i * N_BLOCK, plane_cols[which] + (first + i) * N_BLOCK, out, (first + i) * HEADS, norm)
                 for i in range(count)
@@ -127,8 +130,6 @@ def tile_rawkvinjector_pa_kernel(
 
         load_scales(0)
         nc.sync.dma_start(out=x_all[:, 2, :], in_=x_rows[:, 2, :])
-        nc.sync.dma_start(out=norm_rows[0:1, :HEAD], in_=q_norm_w.unsqueeze(0))
-        nc.sync.dma_start(out=norm_rows[0:1, HEAD:], in_=k_norm_w.unsqueeze(0))
         b0, b1 = load_words(0, 0, 2, 1)
         (b2,) = load_words(0, 2, 1, 2)
         (b3,) = load_words(0, 3, 1, 4)
@@ -295,8 +296,8 @@ def tile_rawkvinjector_pa_kernel(
                     op1=ALU.mult,
                 )
 
-        def rope_sum(block, m, terms, h0=0, h1=HEADS):
-            nc.gpsimd.tensor_tensor(
+        def rope_sum(block, m, terms, h0=0, h1=HEADS, engine=nc.gpsimd):
+            engine.tensor_tensor(
                 out=finished[block[2]][:, h0:h1, m, :].rearrange("p h (s j) -> p h s j", s=2),
                 in0=terms[:, h0:h1, 0, :].rearrange("p h (s j) -> p h s j", s=2),
                 in1=terms[:, h0:h1, 1, :].rearrange("p h (s j) -> p h s j", s=2)[:, :, ::-1, :],
@@ -332,10 +333,10 @@ def tile_rawkvinjector_pa_kernel(
             terms = stage.tile([P, HEADS, 2, HEAD], F32, bufs=6, tag="terms")
             rope_heads(block, m, product, rinv, terms, 0, HEADS // 2)
             if next_rms is None:
-                rope_sum(block, m, terms, 0, HEADS // 2)
-                store(block, nc.sync, 0, HEADS // 2)
                 rope_heads(block, m, product, rinv, terms, HEADS // 2, HEADS)
-                rope_sum(block, m, terms, HEADS // 2, HEADS)
+                rope_sum(block, m, terms, 0, HEADS // 2, nc.vector)
+                store(block, nc.sync, 0, HEADS // 2)
+                rope_sum(block, m, terms, HEADS // 2, HEADS, nc.vector)
                 store(block, nc.sync, HEADS // 2, HEADS)
                 return None
             next_rinv = head_rinv(next_rms)

@@ -72,7 +72,7 @@ def tile_rawkvinjector_pa_kernel(
         ln_rows = keep.tile([P, K_PASS], BF16)
         norm_rows = keep.tile([P, 2 * HEAD], BF16)
         norm_w = keep.tile([P, 2, HEAD], F32)
-        w_planes = keep.tile([P, N_ALL], U8, align_bytes=64)
+        w_planes = keep.tile([P, N_ALL], U8, align_bytes=256)
         eps = keep.tile([P, 1], F32)
         pick = keep.tile([P, PASSES], BF16)
         table_warm = keep.tile([P, 1], F32)
@@ -110,7 +110,7 @@ def tile_rawkvinjector_pa_kernel(
 
         def load_words(which, first, count, passes_each):
             words, scales, out, norm = projections[which]
-            tile = keep.tile([P, PASSES, count * N_BLOCK], U32, name="words%d_%d" % (which, first), align_bytes=64)
+            tile = keep.tile([P, PASSES, count * N_BLOCK], U32, name="words%d_%d" % (which, first), align_bytes=256)
             for g in range(0, PASSES, passes_each):
                 nc.sync.dma_start(
                     out=tile[:, g : g + passes_each, :].bitcast(I32),
@@ -156,11 +156,11 @@ def tile_rawkvinjector_pa_kernel(
         x_rinv = keep.tile([P, TILES], F32)
         v_sumsq = keep.tile([P, 1], F32)
         v_share = keep.tile([P, 1], F32)
-        h_words = keep.tile([P, TILES, PASSES, P], U32, align_bytes=64)
-        h_planes = keep.tile([P, TILES, PASSES, P], U8, align_bytes=64)
+        h_words = keep.tile([P, TILES, PASSES, P], U32, align_bytes=256)
+        h_planes = keep.tile([P, TILES, PASSES, P], U8, align_bytes=256)
         grouped = []
         for m in range(TILES):
-            grouped_m = keep.tile([P, PASSES, P, 2], F32, name="grouped%d" % m, align_bytes=64)
+            grouped_m = keep.tile([P, PASSES, P, 2], F32, name="grouped%d" % m, align_bytes=256)
             grouped.append(grouped_m)
 
         def token_rms(m):

from contextlib import ExitStack

import concourse.mybir as mybir
from concourse.masks import make_identity

F32 = mybir.dt.float32
BF16 = mybir.dt.bfloat16
I32 = mybir.dt.int32
U32 = mybir.dt.uint32
U8 = mybir.dt.uint8
FP8X4 = mybir.dt.float8_e4m3fn_x4
ALU = mybir.AluOpType
ACT = mybir.ActivationFunctionType

P = 128
PACK = 4
K_PASS = P * PACK
TOKENS = 384
D_MODEL = 2048
HEAD = 128
HALF = HEAD // 2
EPS = 1e-6
TILES = TOKENS // P
PASSES = D_MODEL // K_PASS
N_BLOCK = 512
HEADS = N_BLOCK // HEAD
N_ALL = 4096
QUADRANT = 32
LIVE = PASSES * 4
S_SHARE = 1280
PAIR = 2

FLOPS = 2 * TOKENS * D_MODEL * N_ALL


def tile_rawkvinjector_pa_kernel(
    tc,
    hidden_states,
    ln1_w,
    Wq_words,
    Wq_scales,
    Wk_words,
    Wk_scales,
    Wv_words,
    Wv_scales,
    q_norm_w,
    k_norm_w,
    cos,
    sin,
    out_0,
    out_1,
    out_2,
):
    nc = tc.nc
    projections = (
        (Wq_words, Wq_scales, out_0, 0),
        (Wk_words, Wk_scales, out_1, 1),
        (Wv_words, Wv_scales, out_2, None),
    )

    with ExitStack() as ctx:
        keep = ctx.enter_context(tc.tile_pool(name="keep", bufs=1))
        stage = ctx.enter_context(tc.tile_pool(name="stage", bufs=2))
        small = ctx.enter_context(tc.tile_pool(name="small", bufs=4))
        results = ctx.enter_context(tc.tile_pool(name="results", bufs=N_ALL // N_BLOCK))
        turned = ctx.enter_context(tc.psum_pool(name="turned", bufs=2))
        sums = ctx.enter_context(tc.psum_pool(name="sums", bufs=6))
        ctx.enter_context(tc.manual_schedule())

        x_all = keep.tile([P, TILES, D_MODEL], BF16)
        x_rows = hidden_states.rearrange("b (p m) k -> p (b m) k", m=TILES)
        ln_rows = keep.tile([P, K_PASS], BF16)
        norm_rows = keep.tile([P, 2 * HEAD], BF16)
        norm_w = keep.tile([P, 2, HEAD], F32)
        w_planes = keep.tile([P, N_ALL], U8, align_bytes=256)
        eps = keep.tile([P, 1], F32)
        pick = keep.tile([P, PASSES], BF16)
        table_warm = keep.tile([P, 1], F32)
        identity = keep.tile([P, P], F32)
        cos_rows = keep.tile([P, TILES, HEAD], BF16)
        sin_rows = keep.tile([P, TILES, HEAD], BF16)

        nc.vector.memset(eps[:], EPS)
        nc.vector.memset(ln_rows[:].bitcast(I32), 0)
        nc.vector.memset(norm_rows[:].bitcast(I32), 0)
        nc.vector.memset(pick[:], 0.0)
        for g in range(PASSES):
            nc.vector.memset(pick[g * QUADRANT : g * QUADRANT + 1, g : g + 1], 1.0)
        nc.vector.memset(w_planes[:].bitcast(I32), 0)
        nc.scalar.activation(out=table_warm[:], in_=eps[:], func=ACT.Sqrt)
        nc.sync.dma_start(out=x_all[:, 0, :S_SHARE], in_=x_rows[:, 0, :S_SHARE])
        nc.sync.dma_start(out=x_all[:, 0, S_SHARE:], in_=x_rows[:, 0, S_SHARE:])
        nc.sync.dma_start(out=ln_rows[0:P:QUADRANT, :], in_=ln1_w.rearrange("(g n) -> g n", g=PASSES))
        nc.sync.dma_start(out=x_all[:, 1, :], in_=x_rows[:, 1, :])
        nc.gpsimd.dma_start(out=cos_rows[:], in_=cos.rearrange("(p m) d -> p m d", m=TILES))
        nc.gpsimd.dma_start(out=sin_rows[:], in_=sin.rearrange("(p m) d -> p m d", m=TILES))
        make_identity(nc, identity[:])

        plane_cols = (0, Wq_words.shape[2], Wq_words.shape[2] + Wk_words.shape[2])

        def load_scales(which):
            scales, n_cols = projections[which][1], projections[which][1].shape[2]
            for quad in range(P // QUADRANT):
                nc.sync.dma_start(
                    out=w_planes[
                        quad * QUADRANT : quad * QUADRANT + LIVE, plane_cols[which] : plane_cols[which] + n_cols
                    ].bitcast(I32),
                    in_=scales[:, 4 * quad : 4 * quad + 4, :].bitcast(I32),
                )

        def load_words(which, first, count, passes_each):
            words, scales, out, norm = projections[which]
            tile = keep.tile([P, PASSES, count * N_BLOCK], U32, name="words%d_%d" % (which, first), align_bytes=256)
            for g in range(0, PASSES, passes_each):
                nc.sync.dma_start(
                    out=tile[:, g : g + passes_each, :].bitcast(I32),
                    in_=words[g : g + passes_each]
                    .rearrange("g p n t -> p g (n t)")[
                        :, :, PACK * first * N_BLOCK : PACK * (first + count) * N_BLOCK
                    ]
                    .bitcast(I32),
                )
                if which == 0 and first == 0 and g == 0:
                    nc.sync.dma_start(out=norm_rows[0:1, :HEAD], in_=q_norm_w.unsqueeze(0))
                    nc.sync.dma_start(out=norm_rows[0:1, HEAD:], in_=k_norm_w.unsqueeze(0))
            return [
                (tile, i * N_BLOCK, plane_cols[which] + (first + i) * N_BLOCK, out, (first + i) * HEADS, norm)
                for i in range(count)
            ]

        load_scales(0)
        nc.sync.dma_start(out=x_all[:, 2, :], in_=x_rows[:, 2, :])
        b0, b1 = load_words(0, 0, 2, 1)
        (b2,) = load_words(0, 2, 1, 2)
        (b3,) = load_words(0, 3, 1, 4)
        load_scales(1)
        k0, k1 = load_words(1, 0, 2, 2)
        load_scales(2)
        v0, v1 = load_words(2, 0, 2, 2)

        ln_bank = []
        for first in range(0, PASSES, 2):
            spread = sums.tile([P, 2 * K_PASS], BF16, tag="product")
            for i in range(2):
                nc.tensor.matmul(
                    out=spread[:, i * K_PASS : (i + 1) * K_PASS],
                    lhsT=pick[:, first + i : first + i + 1].to_broadcast([P, P]),
                    rhs=ln_rows[:],
                    start=True,
                    stop=True,
                )
            ln_bank.append(spread)

        x_sumsq = keep.tile([P, TILES], F32)
        x_rms = keep.tile([P, TILES], F32)
        x_rinv = keep.tile([P, TILES], F32)
        v_sumsq = keep.tile([P, 1], F32)
        v_share = keep.tile([P, 1], F32)
        h_words = keep.tile([P, TILES, PASSES, P], U32, align_bytes=256)
        h_planes = keep.tile([P, TILES, PASSES, P], U8, align_bytes=256)
        grouped = []
        for m in range(TILES):
            grouped_m = keep.tile([P, PASSES, P, 2], F32, name="grouped%d" % m, align_bytes=256)
            grouped.append(grouped_m)

        def token_rms(m):
            s_cols = S_SHARE if m == 0 else D_MODEL
            squares = stage.tile([P, D_MODEL], BF16)
            nc.scalar.activation(
                out=squares[:, :s_cols], in_=x_all[:, m, :s_cols], func=ACT.Square, accum_out=x_sumsq[:, m : m + 1]
            )
            if m == 0:
                v_squares = stage.tile([P, D_MODEL - S_SHARE], BF16)
                nc.vector.scalar_tensor_tensor(
                    out=v_squares[:],
                    in0=x_all[:, m, s_cols:],
                    scalar=1.0,
                    in1=x_all[:, m, s_cols:],
                    op0=ALU.mult,
                    op1=ALU.mult,
                    accum_out=v_sumsq[:],
                )
                nc.vector.tensor_scalar(
                    out=v_share[:], in0=v_sumsq[:], scalar1=1.0 / D_MODEL, scalar2=EPS, op0=ALU.mult, op1=ALU.add
                )
            nc.scalar.activation(
                out=x_rms[:, m : m + 1],
                in_=x_sumsq[:, m : m + 1],
                func=ACT.Sqrt,
                scale=1.0 / D_MODEL,
                bias=v_share[:] if m == 0 else eps[:],
            )

        def token_rinv(m):
            nc.vector.reciprocal(out=x_rinv[:, m : m + 1], in_=x_rms[:, m : m + 1])

        def normalise(m, half, parts=(0, 1), h_sorted=None):
            if h_sorted is None:
                h_sorted = stage.tile([P, 2, 2 * P, 2], BF16, bufs=4)
            k_range = slice(half * 2 * K_PASS, (half + 1) * 2 * K_PASS)
            x_pairs = x_all[:, m, k_range].rearrange("r (q u e) -> r u q e", u=2, e=2)
            ln_pairs = ln_bank[half][:].rearrange("r (q u e) -> r u q e", u=2, e=2)
            for u in parts:
                nc.vector.scalar_tensor_tensor(
                    out=h_sorted[:, u],
                    in0=x_pairs[:, u],
                    scalar=x_rinv[:, m : m + 1],
                    in1=ln_pairs[:, u],
                    op0=ALU.mult,
                    op1=ALU.mult,
                )
            return h_sorted

        def flip(h_sorted):
            flipped = turned.tile([P, 2, 2, P], F32)
            for i in range(2):
                for u in range(2):
                    words = h_sorted[:, u, i * P : (i + 1) * P, :].rearrange("r q e -> r (q e)")
                    nc.tensor.transpose(flipped[:, i, u, :], words.bitcast(F32), identity[:])
            return flipped

        def group(m, half, flipped):
            nc.scalar.copy(
                out=grouped[m][:, 2 * half : 2 * half + 2], in_=flipped[:].rearrange("p i u r -> p i r u")
            )

        def quantise(m, g0, g1):
            nc.vector.quantize_mx(
                out=h_words[:, m, g0:g1].rearrange("p g c -> p (g c)").bitcast(FP8X4),
                scales=h_planes[:, m, g0:g1].rearrange("p g c -> p (g c)"),
                in_=grouped[m][:, g0:g1].rearrange("p g r u -> p (g r u)").bitcast(BF16),
            )

        def spread_norms():
            norm_bank = sums.tile([P, 2 * HEAD], F32, tag="product")
            nc.tensor.matmul(
                out=norm_bank[:], lhsT=pick[:, 0:1].to_broadcast([P, P]), rhs=norm_rows[:], start=True, stop=True
            )
            nc.scalar.copy(out=norm_w[:].rearrange("p n d -> p (n d)"), in_=norm_bank[:])

        finished = {}
        opened = []

        def open_bank(block, m):
            if len(opened) >= TILES * PAIR and len(opened) % 4 == 1:
                product = turned.tile([P, HEADS, HEAD], F32, tag="flipped")
            else:
                product = sums.tile([P, HEADS, HEAD], F32)
            opened.append(product)
            if block[2] not in finished:
                result = results.tile([P, HEADS, TILES, HEAD], F32)
                finished[block[2]] = result
            return product

        def passes(block, m, product, g0, g1, h0=0, h1=HEADS):
            w_words, words_col, plane_col = block[0], block[1] + h0 * HEAD, block[2] + h0 * HEAD
            n = (h1 - h0) * HEAD
            for g in range(g0, g1):
                nc.tensor.matmul_mx(
                    out=product[:, : h1 - h0, :].rearrange("p h d -> p (h d)"),
                    lhsT=h_words[:, m, g, :].bitcast(FP8X4),
                    lhsT_scale=h_planes[:, m, g, :],
                    rhs=w_words[:, g, words_col : words_col + n].bitcast(FP8X4),
                    rhs_scale=w_planes[4 * g : P, plane_col : plane_col + n],
                    start=(g == 0),
                    stop=(g == PASSES - 1),
                )

        def head_rms(product):
            head_sumsq = small.tile([P, HEADS], F32)
            head_squares = stage.tile([P, HEADS, HEAD], BF16)
            for h in range(HEADS):
                nc.scalar.activation(
                    out=head_squares[:, h, :],
                    in_=product[:, h, :],
                    func=ACT.Square,
                    accum_out=head_sumsq[:, h : h + 1],
                )
            rms = small.tile([P, HEADS], F32)
            nc.scalar.activation(out=rms[:], in_=head_sumsq[:], func=ACT.Sqrt, scale=1.0 / HEAD, bias=eps[:])
            return rms

        def head_rinv(rms):
            rinv = small.tile([P, HEADS], F32)
            nc.vector.reciprocal(out=rinv[:], in_=rms[:])
            return rinv

        def rope_heads(block, m, product, rinv, terms, h0, h1):
            for h in range(h0, h1):
                nc.vector.scalar_tensor_tensor(
                    out=terms[:, h],
                    in0=product[:, h, :].unsqueeze(1).to_broadcast([P, 2, HEAD]),
                    scalar=rinv[:, h : h + 1],
                    in1=rope[:, m, block[5]],
                    op0=ALU.mult,
                    op1=ALU.mult,
                )

        def rope_sum(block, m, terms, h0=0, h1=HEADS, engine=nc.gpsimd):
            engine.tensor_tensor(
                out=finished[block[2]][:, h0:h1, m, :].rearrange("p h (s j) -> p h s j", s=2),
                in0=terms[:, h0:h1, 0, :].rearrange("p h (s j) -> p h s j", s=2),
                in1=terms[:, h0:h1, 1, :].rearrange("p h (s j) -> p h s j", s=2)[:, :, ::-1, :],
                op=ALU.add,
            )

        def store(block, queue, h0=0, h1=HEADS):
            out, first_head = block[3], block[4]
            queue.dma_start(
                out=out.rearrange("b h (p m) d -> p (b h) (m d)", m=TILES)[:, first_head + h0 : first_head + h1, :],
                in_=finished[block[2]][:, h0:h1].rearrange("p h m d -> p h (m d)"),
            )

        minus_w = keep.tile([P, 2, HALF], F32)
        rope = keep.tile([P, TILES, 2, 2, HEAD], F32)

        def make_tables():
            nc.gpsimd.tensor_scalar(
                out=minus_w[:], in0=norm_w[:, :, HALF:], scalar1=-1.0, scalar2=0.0, op0=ALU.mult, op1=ALU.add
            )
            for norm in range(2):
                for out, in0, in1, width in (
                    (rope[:, :, norm, 0, :], cos_rows[:], norm_w[:, norm, :], HEAD),
                    (rope[:, :, norm, 1, :HALF], sin_rows[:, :, HALF:], norm_w[:, norm, :HALF], HALF),
                    (rope[:, :, norm, 1, HALF:], sin_rows[:, :, :HALF], minus_w[:, norm, :], HALF),
                ):
                    nc.gpsimd.tensor_tensor(
                        out=out, in0=in0, in1=in1.unsqueeze(1).to_broadcast([P, TILES, width]), op=ALU.mult
                    )

        def finish(step, next_rms):
            block, m, product, rinv = step
            terms = stage.tile([P, HEADS, 2, HEAD], F32, bufs=6, tag="terms")
            rope_heads(block, m, product, rinv, terms, 0, HEADS // 2)
            if next_rms is None:
                rope_heads(block, m, product, rinv, terms, HEADS // 2, HEADS)
                rope_sum(block, m, terms, 0, HEADS // 2, nc.vector)
                store(block, nc.sync, 0, HEADS // 2)
                rope_sum(block, m, terms, HEADS // 2, HEADS, nc.vector)
                store(block, nc.sync, HEADS // 2, HEADS)
                return None
            next_rinv = head_rinv(next_rms)
            rope_heads(block, m, product, rinv, terms, HEADS // 2, HEADS)
            rope_sum(block, m, terms)
            if m == TILES - 1:
                store(block, nc.sync)
            return next_rinv

        token_rms(0)
        token_rinv(0)
        token_rms(1)
        sorted00 = normalise(0, 0)
        flipped00 = flip(sorted00)
        sorted01 = normalise(0, 1)
        flipped01 = flip(sorted01)
        group(0, 0, flipped00)
        token_rinv(1)
        sorted10 = normalise(1, 0, (0,))
        quantise(0, 0, 2)
        group(0, 1, flipped01)
        token_rms(2)
        spread_norms()
        make_tables()
        p00 = open_bank(b0, 0)
        p10 = open_bank(b1, 0)
        passes(b0, 0, p00, 0, 1)
        passes(b1, 0, p10, 0, 1)
        normalise(1, 0, (1,), sorted10)
        flipped10 = flip(sorted10)
        sorted11 = normalise(1, 1)
        flipped11 = flip(sorted11)
        quantise(0, 2, 4)
        token_rinv(2)
        for g in range(1, PASSES):
            passes(b0, 0, p00, g, g + 1)
            passes(b1, 0, p10, g, g + 1)
        group(1, 0, flipped10)
        group(1, 1, flipped11)
        sorted20 = normalise(2, 0)
        flipped20 = flip(sorted20)
        quantise(1, 0, 4)
        rms00 = head_rms(p00)
        p01 = open_bank(b0, 1)
        passes(b0, 1, p01, 0, 4)
        group(2, 0, flipped20)
        sorted21 = normalise(2, 1)
        flipped21 = flip(sorted21)
        rms10 = head_rms(p10)
        group(2, 1, flipped21)
        p11 = open_bank(b1, 1)
        passes(b1, 1, p11, 0, 4)
        rinv10 = finish((b0, 0, p00, head_rinv(rms00)), rms10)
        rms01 = head_rms(p01)
        rinv01 = finish((b1, 0, p10, rinv10), rms01)
        quantise(2, 0, 4)
        held = (b0, 1, p01, rinv01)
        rms11 = head_rms(p11)
        held = (b1, 1, p11, finish(held, rms11))

        steps = [(b2, 0), (b2, 1), (b0, 2), (b1, 2), (b2, 2)]
        for block in (b3, k0, v0, k1):
            for m in range(TILES):
                steps.append((block, m))
        for block, m in steps:
            product = open_bank(block, m)
            passes(block, m, product, 0, PASSES)
            if block[5] is None:
                nc.scalar.copy(out=finished[block[2]][:, :, m, :], in_=product[:])
                if m == TILES - 1:
                    store(block, nc.scalar)
            else:
                rms = head_rms(product)
                held = (block, m, product, finish(held, rms))
        finish(held, None)
        for h0 in range(0, HEADS, HEADS // 2):
            h1 = h0 + HEADS // 2
            for m in range(TILES):
                product = open_bank(v1, m)
                passes(v1, m, product, 0, PASSES, h0, h1)
                nc.scalar.copy(out=finished[v1[2]][:, h0:h1, m, :], in_=product[:, : h1 - h0, :])
            store(v1, nc.scalar, h0, h1)
